import numpy as np
import ml_dtypes

BF16 = ml_dtypes.bfloat16


def bf(x):
    return np.asarray(x, np.float32).astype(BF16)


def f32(x):
    return np.asarray(x, np.float32)


def f64(x):
    return np.asarray(x).astype(np.float64)


def striped(idx):
    return np.tile(idx.reshape(-1, 16).T, (8, 1))


D, T, C, S, P, NB, N, H, DPH, RUN, RUNS = 128, 3, 384, 512, 128, 16, 2048, 8, 16, 256, 8


def setup_inputs():
    v = f32(np.random.standard_normal((C, S)))
    dist = f32(np.repeat(2.0 * np.random.standard_normal((H, N)), DPH, axis=0))
    wo = bf(np.random.standard_normal((D, D)) / np.sqrt(D))
    tgt = f32(np.random.standard_normal((C, P)))
    idx = np.concatenate([np.random.permutation(S)[:RUN] for _ in range(RUNS)])
    return {"v": v, "dist": dist, "wo": wo, "tgt": tgt, "offs": striped(idx)}


def reference(v, dist, wo, tgt, offs):
    idx = offs[:16].T.reshape(-1)
    e = np.exp(f64(dist) / np.sqrt(DPH)).reshape(D, P, NB)
    att = (e / e.sum(axis=2, keepdims=True)).reshape(D, N)
    picked = f64(v)[:, idx].reshape(T, D, N) * att[None, :, :]
    agg = picked.reshape(T, D, P, NB).sum(axis=3)
    proj = np.einsum('do,tdp->top', f64(wo), agg)
    return f64(tgt) + proj.reshape(C, P)

@@ -1,0 +1,82 @@
+import concourse.mybir as mybir
+
+F32, BF16, U16 = mybir.dt.float32, mybir.dt.bfloat16, mybir.dt.uint16
+ALU = mybir.AluOpType
+X = mybir.AxisListType.X
+EXP = mybir.ActivationFunctionType.Exp
+
+D = 128
+T = 3
+S = 512
+P = 128
+NB = 16
+N = P * NB
+PIECE = 512
+PIECES = N // PIECE
+PTS = PIECE // NB
+COLS = PIECE // 16
+
+FLOPS = 2 * T * D * N + 2 * D * D * T * P
+
+
+def tile_transformerdecoderlayer_equi_v4_kernel(tc, v, dist, wo, tgt, offs, out):
+    nc = tc.nc
+    with (
+        tc.tile_pool(name="held", bufs=1) as held,
+        tc.tile_pool(name="work", bufs=2) as work,
+        tc.psum_pool(name="psum", bufs=1) as psum,
+    ):
+        offsets = held.tile([D, N // 16], U16, name="offsets")
+        nc.sync.dma_start(offsets[:], offs)
+        logits = [held.tile([D, PTS, NB], F32, name=f"logits{k}") for k in range(PIECES)]
+        values = [held.tile([D, S], F32, name=f"values{t}") for t in range(T)]
+        nc.scalar.dma_start(logits[0][:], dist[:, 0:PIECE].rearrange("d (p n) -> d p n", n=NB))
+        nc.sync.dma_start(values[0][:], v[0:D, :])
+        nc.scalar.dma_start(values[1][:], v[D : 2 * D, :])
+        nc.sync.dma_start(values[2][:], v[2 * D : 3 * D, :])
+        for k in range(1, PIECES):
+            queue = nc.scalar if k % 2 else nc.sync
+            queue.dma_start(
+                logits[k][:], dist[:, k * PIECE : (k + 1) * PIECE].rearrange("d (p n) -> d p n", n=NB)
+            )
+        weights = held.tile([D, D], BF16, name="weights")
+        nc.scalar.dma_start(weights[:], wo)
+        own = held.tile([D, T, P], F32, name="own")
+        nc.sync.dma_start(own[:], tgt.rearrange("(t o) p -> o t p", o=D))
+
+        agg = held.tile([D, T, P], BF16, name="agg")
+
+        for k in range(PIECES):
+            points = slice(k * PTS, (k + 1) * PTS)
+            peak = work.tile([D, PTS], F32, name="peak")
+            nc.vector.tensor_reduce(out=peak[:], in_=logits[k][:], axis=X, op=ALU.max)
+            shifted = work.tile([D, PTS, NB], F32, name="shifted")
+            nc.vector.tensor_tensor(
+                shifted[:], logits[k][:], peak[:].unsqueeze(2).to_broadcast([D, PTS, NB]), ALU.subtract
+            )
+            weight = work.tile([D, PTS, NB], F32, name="weight")
+            nc.scalar.activation(weight[:], shifted[:], EXP, scale=0.25)
+            total = work.tile([D, PTS], F32, name="total")
+            nc.vector.tensor_reduce(out=total[:], in_=weight[:], axis=X, op=ALU.add)
+            inverse = work.tile([D, PTS], F32, name="inverse")
+            nc.vector.reciprocal(inverse[:], total[:])
+
+            for t in range(T):
+                product = work.tile([D, PTS, NB], F32, name="product")
+                nc.vector.tensor_tensor(
+                    product[:].rearrange("d p n -> d (p n)"),
+                    values[t][:].indirect(offsets[:, k * COLS : (k + 1) * COLS]),
+                    weight[:].rearrange("d p n -> d (p n)"),
+                    ALU.mult,
+                )
+                summed = work.tile([D, PTS], F32, name="summed")
+                nc.vector.tensor_reduce(out=summed[:], in_=product[:], axis=X, op=ALU.add)
+                nc.vector.tensor_tensor(agg[:, t, points], summed[:], inverse[:], ALU.mult)
+
+        projected = psum.tile([D, T, P], F32, name="projected")
+        nc.tensor.matmul(
+            projected[:].rearrange("o t p -> o (t p)"), weights[:], agg[:].rearrange("d t p -> d (t p)")
+        )
+        result = held.tile([D, T, P], F32, name="result")
+        nc.vector.tensor_tensor(result[:], projected[:], own[:], ALU.add)
+        nc.sync.dma_start(out.rearrange("(t o) p -> o t p", o=D), result[:])

@@ -1,4 +1,5 @@
 import concourse.mybir as mybir
+from concourse.masks import make_identity
 
 F32, BF16, U16 = mybir.dt.float32, mybir.dt.bfloat16, mybir.dt.uint16
 ALU = mybir.AluOpType
@@ -12,9 +13,11 @@ P = 128
 NB = 16
 N = P * NB
 PIECE = 512
-PIECES = N // PIECE
 PTS = PIECE // NB
 COLS = PIECE // 16
+PAIR = 2
+BATCHES = N // (PAIR * PIECE)
+BPTS = PAIR * PTS
 
 FLOPS = 2 * T * D * N + 2 * D * D * T * P
 
@@ -24,59 +27,76 @@ def tile_transformerdecoderlayer_equi_v4_kernel(tc, v, dist, wo, tgt, offs, out)
     with (
         tc.tile_pool(name="held", bufs=1) as held,
         tc.tile_pool(name="work", bufs=2) as work,
-        tc.psum_pool(name="psum", bufs=1) as psum,
+        tc.tile_pool(name="products", bufs=3) as products,
+        tc.psum_pool(name="psum", bufs=2) as psum,
     ):
         offsets = held.tile([D, N // 16], U16, name="offsets")
         nc.sync.dma_start(offsets[:], offs)
-        logits = [held.tile([D, PTS, NB], F32, name=f"logits{k}") for k in range(PIECES)]
+        logits = [held.tile([D, PTS, NB], F32, name=f"logits{k}") for k in range(N // PIECE)]
         values = [held.tile([D, S], F32, name=f"values{t}") for t in range(T)]
-        nc.scalar.dma_start(logits[0][:], dist[:, 0:PIECE].rearrange("d (p n) -> d p n", n=NB))
-        nc.sync.dma_start(values[0][:], v[0:D, :])
-        nc.scalar.dma_start(values[1][:], v[D : 2 * D, :])
-        nc.sync.dma_start(values[2][:], v[2 * D : 3 * D, :])
-        for k in range(1, PIECES):
-            queue = nc.scalar if k % 2 else nc.sync
-            queue.dma_start(
-                logits[k][:], dist[:, k * PIECE : (k + 1) * PIECE].rearrange("d (p n) -> d p n", n=NB)
-            )
+        pieces_of_dist = dist.rearrange("d (k p n) -> k d p n", p=PTS, n=NB)
+        nc.scalar.dma_start(logits[0][:], pieces_of_dist[0])
+        nc.sync.dma_start(logits[1][:], pieces_of_dist[1])
+        nc.scalar.dma_start(values[0][:], v[0:D, :])
+        nc.sync.dma_start(values[1][:], v[D : 2 * D, :])
+        nc.scalar.dma_start(values[2][:], v[2 * D : 3 * D, :])
+        nc.sync.dma_start(logits[2][:], pieces_of_dist[2])
+        nc.scalar.dma_start(logits[3][:], pieces_of_dist[3])
         weights = held.tile([D, D], BF16, name="weights")
-        nc.scalar.dma_start(weights[:], wo)
+        nc.sync.dma_start(weights[:], wo)
         own = held.tile([D, T, P], F32, name="own")
-        nc.sync.dma_start(own[:], tgt.rearrange("(t o) p -> o t p", o=D))
+        nc.scalar.dma_start(own[:], tgt.rearrange("(t o) p -> o t p", o=D))
 
-        agg = held.tile([D, T, P], BF16, name="agg")
+        identity = held.tile([D, D], F32, name="identity")
+        make_identity(nc, identity[:])
 
-        for k in range(PIECES):
-            points = slice(k * PTS, (k + 1) * PTS)
-            peak = work.tile([D, PTS], F32, name="peak")
-            nc.vector.tensor_reduce(out=peak[:], in_=logits[k][:], axis=X, op=ALU.max)
-            shifted = work.tile([D, PTS, NB], F32, name="shifted")
-            nc.vector.tensor_tensor(
-                shifted[:], logits[k][:], peak[:].unsqueeze(2).to_broadcast([D, PTS, NB]), ALU.subtract
-            )
-            weight = work.tile([D, PTS, NB], F32, name="weight")
-            nc.scalar.activation(weight[:], shifted[:], EXP, scale=0.25)
-            total = work.tile([D, PTS], F32, name="total")
-            nc.vector.tensor_reduce(out=total[:], in_=weight[:], axis=X, op=ALU.add)
-            inverse = work.tile([D, PTS], F32, name="inverse")
+        zero = held.tile([D, 1], F32, name="zero")
+        nc.vector.memset(zero[:], 0.0)
+        one = held.tile([D, 1], F32, name="one")
+        nc.scalar.activation(one[:], zero[:], EXP)
+
+        def sum_neighbours(sums, terms):
+            for n in range(NB):
+                nc.tensor.matmul(sums, identity[:], terms[:, :, n], start=(n == 0), stop=(n == NB - 1))
+
+        for b in range(BATCHES):
+            weight = work.tile([D, BPTS, NB], F32, name="weight")
+            for k in range(PAIR * b, PAIR * (b + 1)):
+                peak = work.tile([D, PTS], F32, name="peak")
+                nc.vector.tensor_reduce(out=peak[:], in_=logits[k][:], axis=X, op=ALU.max)
+                shifted = work.tile([D, PTS, NB], F32, name="shifted")
+                nc.vector.tensor_tensor(
+                    shifted[:], logits[k][:], peak[:].unsqueeze(2).to_broadcast([D, PTS, NB]), ALU.subtract
+                )
+                first = (k % PAIR) * PTS
+                nc.scalar.activation(weight[:, first : first + PTS, :], shifted[:], EXP, scale=0.25)
+            total = psum.tile([D, BPTS], F32, name="total")
+            sum_neighbours(total[:], weight)
+            inverse = work.tile([D, BPTS], F32, name="inverse")
             nc.vector.reciprocal(inverse[:], total[:])
 
+            summed = psum.tile([D, T, BPTS], F32, name="summed")
             for t in range(T):
-                product = work.tile([D, PTS, NB], F32, name="product")
-                nc.vector.tensor_tensor(
-                    product[:].rearrange("d p n -> d (p n)"),
-                    values[t][:].indirect(offsets[:, k * COLS : (k + 1) * COLS]),
-                    weight[:].rearrange("d p n -> d (p n)"),
-                    ALU.mult,
-                )
-                summed = work.tile([D, PTS], F32, name="summed")
-                nc.vector.tensor_reduce(out=summed[:], in_=product[:], axis=X, op=ALU.add)
-                nc.vector.tensor_tensor(agg[:, t, points], summed[:], inverse[:], ALU.mult)
+                product = products.tile([D, BPTS, NB], F32, name="product")
+                for k in range(PAIR * b, PAIR * (b + 1)):
+                    first = (k % PAIR) * PTS
+                    nc.vector.tensor_tensor(
+                        product[:, first : first + PTS, :].rearrange("d p n -> d (p n)"),
+                        values[t][:].indirect(offsets[:, k * COLS : (k + 1) * COLS]),
+                        weight[:, first : first + PTS, :].rearrange("d p n -> d (p n)"),
+                        ALU.mult,
+                    )
+                sum_neighbours(summed[:, t, :], product)
 
-        projected = psum.tile([D, T, P], F32, name="projected")
-        nc.tensor.matmul(
-            projected[:].rearrange("o t p -> o (t p)"), weights[:], agg[:].rearrange("d t p -> d (t p)")
-        )
-        result = held.tile([D, T, P], F32, name="result")
-        nc.vector.tensor_tensor(result[:], projected[:], own[:], ALU.add)
-        nc.sync.dma_start(out.rearrange("(t o) p -> o t p", o=D), result[:])
+            agg = work.tile([D, T, BPTS], BF16, name="agg")
+            nc.vector.tensor_tensor(
+                agg[:], summed[:], inverse[:].unsqueeze(1).to_broadcast([D, T, BPTS]), ALU.mult
+            )
+            projected = psum.tile([D, T, BPTS], F32, name="projected")
+            nc.tensor.matmul(
+                projected[:].rearrange("o t p -> o (t p)"), weights[:], agg[:].rearrange("d t p -> d (t p)")
+            )
+            points = slice(b * BPTS, (b + 1) * BPTS)
+            result = work.tile([D, T, BPTS], F32, name="result")
+            nc.vector.tensor_tensor(result[:], projected[:], own[:, :, points], ALU.add)
+            nc.sync.dma_start(out.rearrange("(t o) p -> o t p", o=D)[:, :, points], result[:])

@@ -13,11 +13,9 @@ P = 128
 NB = 16
 N = P * NB
 PIECE = 512
+PIECES = N // PIECE
 PTS = PIECE // NB
 COLS = PIECE // 16
-PAIR = 2
-BATCHES = N // (PAIR * PIECE)
-BPTS = PAIR * PTS
 
 FLOPS = 2 * T * D * N + 2 * D * D * T * P
 
@@ -27,12 +25,11 @@ def tile_transformerdecoderlayer_equi_v4_kernel(tc, v, dist, wo, tgt, offs, out)
     with (
         tc.tile_pool(name="held", bufs=1) as held,
         tc.tile_pool(name="work", bufs=2) as work,
-        tc.tile_pool(name="products", bufs=3) as products,
         tc.psum_pool(name="psum", bufs=2) as psum,
     ):
         offsets = held.tile([D, N // 16], U16, name="offsets")
         nc.sync.dma_start(offsets[:], offs)
-        logits = [held.tile([D, PTS, NB], F32, name=f"logits{k}") for k in range(N // PIECE)]
+        logits = [held.tile([D, PTS, NB], F32, name=f"logits{k}") for k in range(PIECES)]
         values = [held.tile([D, S], F32, name=f"values{t}") for t in range(T)]
         pieces_of_dist = dist.rearrange("d (k p n) -> k d p n", p=PTS, n=NB)
         nc.scalar.dma_start(logits[0][:], pieces_of_dist[0])
@@ -55,48 +52,59 @@ def tile_transformerdecoderlayer_equi_v4_kernel(tc, v, dist, wo, tgt, offs, out)
         one = held.tile([D, 1], F32, name="one")
         nc.scalar.activation(one[:], zero[:], EXP)
 
-        def sum_neighbours(sums, terms):
-            for n in range(NB):
-                nc.tensor.matmul(sums, identity[:], terms[:, :, n], start=(n == 0), stop=(n == NB - 1))
+        terms = [held.tile([D, T + 1, PTS, NB], F32, name=f"terms{k}") for k in range(PIECES)]
+        sums = [None] * PIECES
 
-        for b in range(BATCHES):
-            weight = work.tile([D, BPTS, NB], F32, name="weight")
-            for k in range(PAIR * b, PAIR * (b + 1)):
-                peak = work.tile([D, PTS], F32, name="peak")
-                nc.vector.tensor_reduce(out=peak[:], in_=logits[k][:], axis=X, op=ALU.max)
-                shifted = work.tile([D, PTS, NB], F32, name="shifted")
-                nc.vector.tensor_tensor(
-                    shifted[:], logits[k][:], peak[:].unsqueeze(2).to_broadcast([D, PTS, NB]), ALU.subtract
-                )
-                first = (k % PAIR) * PTS
-                nc.scalar.activation(weight[:, first : first + PTS, :], shifted[:], EXP, scale=0.25)
-            total = psum.tile([D, BPTS], F32, name="total")
-            sum_neighbours(total[:], weight)
-            inverse = work.tile([D, BPTS], F32, name="inverse")
-            nc.vector.reciprocal(inverse[:], total[:])
-
-            summed = psum.tile([D, T, BPTS], F32, name="summed")
-            for t in range(T):
-                product = products.tile([D, BPTS, NB], F32, name="product")
-                for k in range(PAIR * b, PAIR * (b + 1)):
-                    first = (k % PAIR) * PTS
-                    nc.vector.tensor_tensor(
-                        product[:, first : first + PTS, :].rearrange("d p n -> d (p n)"),
-                        values[t][:].indirect(offsets[:, k * COLS : (k + 1) * COLS]),
-                        weight[:, first : first + PTS, :].rearrange("d p n -> d (p n)"),
-                        ALU.mult,
-                    )
-                sum_neighbours(summed[:, t, :], product)
-
-            agg = work.tile([D, T, BPTS], BF16, name="agg")
+        def weigh(k):
+            peak = work.tile([D, PTS], F32, name="peak")
+            nc.vector.tensor_reduce(out=peak[:], in_=logits[k][:], axis=X, op=ALU.max)
+            shifted = work.tile([D, PTS, NB], F32, name="shifted")
             nc.vector.tensor_tensor(
-                agg[:], summed[:], inverse[:].unsqueeze(1).to_broadcast([D, T, BPTS]), ALU.mult
+                shifted[:], logits[k][:], peak[:].unsqueeze(2).to_broadcast([D, PTS, NB]), ALU.subtract
             )
-            projected = psum.tile([D, T, BPTS], F32, name="projected")
+            nc.scalar.activation(terms[k][:, T], shifted[:], EXP, scale=0.25)
+
+        def look_up_and_sum(k):
+            for t in range(T):
+                nc.vector.tensor_tensor(
+                    terms[k][:, t].rearrange("d p n -> d (p n)"),
+                    values[t][:].indirect(offsets[:, k * COLS : (k + 1) * COLS]),
+                    terms[k][:, T].rearrange("d p n -> d (p n)"),
+                    ALU.mult,
+                )
+            by_neighbour = terms[k][:].rearrange("d t p n -> d (t p) n")
+            flipped = psum.tile([(T + 1) * PTS, D], F32, name="flipped")
+            for n in range(NB):
+                nc.tensor.matmul(
+                    flipped[:], by_neighbour[:, :, n], identity[:], is_transpose=True, start=(n == 0), stop=(n == NB - 1)
+                )
+            flipped_sb = work.tile([(T + 1) * PTS, D], F32, name="flipped_sb")
+            nc.scalar.copy(flipped_sb[:], flipped[:])
+            sums[k] = psum.tile([D, T + 1, PTS], F32, name="sums")
+            nc.tensor.transpose(sums[k][:].rearrange("d t p -> d (t p)"), flipped_sb[:], identity[:])
+
+        def finish(k):
+            inverse = work.tile([D, PTS], F32, name="inverse")
+            nc.vector.reciprocal(inverse[:], sums[k][:, T])
+            agg = work.tile([D, T, PTS], BF16, name="agg")
+            nc.vector.tensor_tensor(
+                agg[:], sums[k][:, 0:T], inverse[:].unsqueeze(1).to_broadcast([D, T, PTS]), ALU.mult
+            )
+            projected = psum.tile([D, T, PTS], F32, name="projected")
             nc.tensor.matmul(
                 projected[:].rearrange("o t p -> o (t p)"), weights[:], agg[:].rearrange("d t p -> d (t p)")
             )
-            points = slice(b * BPTS, (b + 1) * BPTS)
-            result = work.tile([D, T, BPTS], F32, name="result")
+            points = slice(k * PTS, (k + 1) * PTS)
+            result = work.tile([D, T, PTS], F32, name="result")
             nc.vector.tensor_tensor(result[:], projected[:], own[:, :, points], ALU.add)
             nc.sync.dma_start(out.rearrange("(t o) p -> o t p", o=D)[:, :, points], result[:])
+
+        weigh(0)
+        weigh(1)
+        for k in range(PIECES):
+            look_up_and_sum(k)
+            if k + 2 < PIECES:
+                weigh(k + 2)
+            if k >= 1:
+                finish(k - 1)
+        finish(PIECES - 1)

@@ -11,6 +11,8 @@ T = 3
 S = 512
 P = 128
 NB = 16
+H = 8
+DPH = D // H
 N = P * NB
 PIECE = 512
 PIECES = N // PIECE
@@ -26,23 +28,26 @@ def tile_transformerdecoderlayer_equi_v4_kernel(tc, v, dist, wo, tgt, offs, out)
         tc.tile_pool(name="held", bufs=1) as held,
         tc.tile_pool(name="work", bufs=2) as work,
         tc.psum_pool(name="psum", bufs=2) as psum,
+        tc.psum_pool(name="psum_held", bufs=1) as psum_held,
     ):
-        offsets = held.tile([D, N // 16], U16, name="offsets")
-        nc.sync.dma_start(offsets[:], offs)
+        by_point = held.tile([P, H, NB], F32, name="by_point")
+        nc.sync.dma_start(by_point[:], dist.rearrange("(h r) (p n) -> r p h n", r=DPH, n=NB)[0])
         logits = [held.tile([D, PTS, NB], F32, name=f"logits{k}") for k in range(PIECES)]
         values = [held.tile([D, S], F32, name=f"values{t}") for t in range(T)]
         pieces_of_dist = dist.rearrange("d (k p n) -> k d p n", p=PTS, n=NB)
         nc.scalar.dma_start(logits[0][:], pieces_of_dist[0])
-        nc.sync.dma_start(logits[1][:], pieces_of_dist[1])
+        offsets = held.tile([D, N // 16], U16, name="offsets")
+        nc.sync.dma_start(offsets[:], offs)
         nc.scalar.dma_start(values[0][:], v[0:D, :])
-        nc.sync.dma_start(values[1][:], v[D : 2 * D, :])
-        nc.scalar.dma_start(values[2][:], v[2 * D : 3 * D, :])
-        nc.sync.dma_start(logits[2][:], pieces_of_dist[2])
-        nc.scalar.dma_start(logits[3][:], pieces_of_dist[3])
+        nc.sync.dma_start(logits[1][:], pieces_of_dist[1])
+        nc.scalar.dma_start(values[1][:], v[D : 2 * D, :])
+        nc.sync.dma_start(values[2][:], v[2 * D : 3 * D, :])
+        nc.scalar.dma_start(logits[2][:], pieces_of_dist[2])
+        nc.sync.dma_start(logits[3][:], pieces_of_dist[3])
         weights = held.tile([D, D], BF16, name="weights")
         nc.sync.dma_start(weights[:], wo)
         own = held.tile([D, T, P], F32, name="own")
-        nc.scalar.dma_start(own[:], tgt.rearrange("(t o) p -> o t p", o=D))
+        nc.sync.dma_start(own[:], tgt.rearrange("(t o) p -> o t p", o=D))
 
         identity = held.tile([D, D], F32, name="identity")
         make_identity(nc, identity[:])
@@ -52,26 +57,36 @@ def tile_transformerdecoderlayer_equi_v4_kernel(tc, v, dist, wo, tgt, offs, out)
         one = held.tile([D, 1], F32, name="one")
         nc.scalar.activation(one[:], zero[:], EXP)
 
+        peak_of_head = held.tile([P, H], F32, name="peak_of_head")
+        nc.vector.tensor_reduce(out=peak_of_head[:], in_=by_point[:], axis=X, op=ALU.max)
+        peaks_flipped = held.tile([P, H, DPH], F32, name="peaks_flipped")
+        nc.vector.tensor_copy(peaks_flipped[:], peak_of_head[:].unsqueeze(2).to_broadcast([P, H, DPH]))
+        peaks = psum_held.tile([D, P], F32, name="peaks")
+        nc.tensor.transpose(peaks[:], peaks_flipped[:].rearrange("p h r -> p (h r)"), identity[:])
+
         terms = [held.tile([D, T + 1, PTS, NB], F32, name=f"terms{k}") for k in range(PIECES)]
         sums = [None] * PIECES
+        projected = [None] * PIECES
 
         def weigh(k):
-            peak = work.tile([D, PTS], F32, name="peak")
-            nc.vector.tensor_reduce(out=peak[:], in_=logits[k][:], axis=X, op=ALU.max)
             shifted = work.tile([D, PTS, NB], F32, name="shifted")
             nc.vector.tensor_tensor(
-                shifted[:], logits[k][:], peak[:].unsqueeze(2).to_broadcast([D, PTS, NB]), ALU.subtract
+                shifted[:],
+                logits[k][:],
+                peaks[:, k * PTS : (k + 1) * PTS].unsqueeze(2).to_broadcast([D, PTS, NB]),
+                ALU.subtract,
             )
             nc.scalar.activation(terms[k][:, T], shifted[:], EXP, scale=0.25)
 
-        def look_up_and_sum(k):
-            for t in range(T):
-                nc.vector.tensor_tensor(
-                    terms[k][:, t].rearrange("d p n -> d (p n)"),
-                    values[t][:].indirect(offsets[:, k * COLS : (k + 1) * COLS]),
-                    terms[k][:, T].rearrange("d p n -> d (p n)"),
-                    ALU.mult,
-                )
+        def look_up(k, t):
+            nc.vector.tensor_tensor(
+                terms[k][:, t].rearrange("d p n -> d (p n)"),
+                values[t][:].indirect(offsets[:, k * COLS : (k + 1) * COLS]),
+                terms[k][:, T].rearrange("d p n -> d (p n)"),
+                ALU.mult,
+            )
+
+        def sum_on_tensor(k):
             by_neighbour = terms[k][:].rearrange("d t p n -> d (t p) n")
             flipped = psum.tile([(T + 1) * PTS, D], F32, name="flipped")
             for n in range(NB):
@@ -83,28 +98,42 @@ def tile_transformerdecoderlayer_equi_v4_kernel(tc, v, dist, wo, tgt, offs, out)
             sums[k] = psum.tile([D, T + 1, PTS], F32, name="sums")
             nc.tensor.transpose(sums[k][:].rearrange("d t p -> d (t p)"), flipped_sb[:], identity[:])
 
-        def finish(k):
+        def sum_on_vector(k):
+            sums[k] = work.tile([D, T + 1, PTS], F32, name="sums_sb")
+            nc.vector.tensor_reduce(out=sums[k][:], in_=terms[k][:], axis=X, op=ALU.add)
+
+        def divide_and_project(k):
             inverse = work.tile([D, PTS], F32, name="inverse")
             nc.vector.reciprocal(inverse[:], sums[k][:, T])
             agg = work.tile([D, T, PTS], BF16, name="agg")
             nc.vector.tensor_tensor(
                 agg[:], sums[k][:, 0:T], inverse[:].unsqueeze(1).to_broadcast([D, T, PTS]), ALU.mult
             )
-            projected = psum.tile([D, T, PTS], F32, name="projected")
+            projected[k] = psum.tile([D, T, PTS], F32, name="projected")
             nc.tensor.matmul(
-                projected[:].rearrange("o t p -> o (t p)"), weights[:], agg[:].rearrange("d t p -> d (t p)")
+                projected[k][:].rearrange("o t p -> o (t p)"), weights[:], agg[:].rearrange("d t p -> d (t p)")
             )
+
+        def add_own_and_store(k):
             points = slice(k * PTS, (k + 1) * PTS)
             result = work.tile([D, T, PTS], F32, name="result")
-            nc.vector.tensor_tensor(result[:], projected[:], own[:, :, points], ALU.add)
+            nc.vector.tensor_tensor(result[:], projected[k][:], own[:, :, points], ALU.add)
             nc.sync.dma_start(out.rearrange("(t o) p -> o t p", o=D)[:, :, points], result[:])
 
-        weigh(0)
-        weigh(1)
         for k in range(PIECES):
-            look_up_and_sum(k)
-            if k + 2 < PIECES:
-                weigh(k + 2)
-            if k >= 1:
-                finish(k - 1)
-        finish(PIECES - 1)
+            weigh(k)
+        for k in range(PIECES):
+            look_up(k, 0)
+            if k >= 2:
+                divide_and_project(k - 2)
+            look_up(k, 1)
+            if k >= 2:
+                add_own_and_store(k - 2)
+            look_up(k, 2)
+            if k < PIECES - 1:
+                sum_on_tensor(k)
+        sum_on_vector(PIECES - 1)
+        divide_and_project(PIECES - 2)
+        divide_and_project(PIECES - 1)
+        add_own_and_store(PIECES - 2)
+        add_own_and_store(PIECES - 1)

@@ -45,7 +45,7 @@ def tile_transformerdecoderlayer_equi_v4_kernel(tc, v, dist, wo, tgt, offs, out)
         nc.scalar.dma_start(logits[2][:], pieces_of_dist[2])
         nc.sync.dma_start(logits[3][:], pieces_of_dist[3])
         weights = held.tile([D, D], BF16, name="weights")
-        nc.sync.dma_start(weights[:], wo)
+        nc.scalar.dma_start(weights[:], wo)
         own = held.tile([D, T, P], F32, name="own")
         nc.sync.dma_start(own[:], tgt.rearrange("(t o) p -> o t p", o=D))
 
@@ -120,8 +120,8 @@ def tile_transformerdecoderlayer_equi_v4_kernel(tc, v, dist, wo, tgt, offs, out)
             nc.vector.tensor_tensor(result[:], projected[k][:], own[:, :, points], ALU.add)
             nc.sync.dma_start(out.rearrange("(t o) p -> o t p", o=D)[:, :, points], result[:])
 
-        for k in range(PIECES):
-            weigh(k)
+        weigh(0)
+        weigh(1)
         for k in range(PIECES):
             look_up(k, 0)
             if k >= 2:
@@ -132,6 +132,8 @@ def tile_transformerdecoderlayer_equi_v4_kernel(tc, v, dist, wo, tgt, offs, out)
             look_up(k, 2)
             if k < PIECES - 1:
                 sum_on_tensor(k)
+            if k + 2 < PIECES:
+                weigh(k + 2)
         sum_on_vector(PIECES - 1)
         divide_and_project(PIECES - 2)
         divide_and_project(PIECES - 1)

@@ -11,8 +11,6 @@ T = 3
 S = 512
 P = 128
 NB = 16
-H = 8
-DPH = D // H
 N = P * NB
 PIECE = 512
 PIECES = N // PIECE
@@ -28,26 +26,23 @@ def tile_transformerdecoderlayer_equi_v4_kernel(tc, v, dist, wo, tgt, offs, out)
         tc.tile_pool(name="held", bufs=1) as held,
         tc.tile_pool(name="work", bufs=2) as work,
         tc.psum_pool(name="psum", bufs=2) as psum,
-        tc.psum_pool(name="psum_held", bufs=1) as psum_held,
     ):
-        by_point = held.tile([P, H, NB], F32, name="by_point")
-        nc.sync.dma_start(by_point[:], dist.rearrange("(h r) (p n) -> r p h n", r=DPH, n=NB)[0])
+        offsets = held.tile([D, N // 16], U16, name="offsets")
+        nc.sync.dma_start(offsets[:], offs)
         logits = [held.tile([D, PTS, NB], F32, name=f"logits{k}") for k in range(PIECES)]
         values = [held.tile([D, S], F32, name=f"values{t}") for t in range(T)]
         pieces_of_dist = dist.rearrange("d (k p n) -> k d p n", p=PTS, n=NB)
         nc.scalar.dma_start(logits[0][:], pieces_of_dist[0])
-        offsets = held.tile([D, N // 16], U16, name="offsets")
-        nc.sync.dma_start(offsets[:], offs)
-        nc.scalar.dma_start(values[0][:], v[0:D, :])
         nc.sync.dma_start(logits[1][:], pieces_of_dist[1])
-        nc.scalar.dma_start(values[1][:], v[D : 2 * D, :])
-        nc.sync.dma_start(values[2][:], v[2 * D : 3 * D, :])
-        nc.scalar.dma_start(logits[2][:], pieces_of_dist[2])
-        nc.sync.dma_start(logits[3][:], pieces_of_dist[3])
+        nc.scalar.dma_start(values[0][:], v[0:D, :])
+        nc.sync.dma_start(values[1][:], v[D : 2 * D, :])
+        nc.scalar.dma_start(values[2][:], v[2 * D : 3 * D, :])
+        nc.sync.dma_start(logits[2][:], pieces_of_dist[2])
+        nc.scalar.dma_start(logits[3][:], pieces_of_dist[3])
         weights = held.tile([D, D], BF16, name="weights")
-        nc.scalar.dma_start(weights[:], wo)
+        nc.sync.dma_start(weights[:], wo)
         own = held.tile([D, T, P], F32, name="own")
-        nc.sync.dma_start(own[:], tgt.rearrange("(t o) p -> o t p", o=D))
+        nc.scalar.dma_start(own[:], tgt.rearrange("(t o) p -> o t p", o=D))
 
         identity = held.tile([D, D], F32, name="identity")
         make_identity(nc, identity[:])
@@ -57,24 +52,16 @@ def tile_transformerdecoderlayer_equi_v4_kernel(tc, v, dist, wo, tgt, offs, out)
         one = held.tile([D, 1], F32, name="one")
         nc.scalar.activation(one[:], zero[:], EXP)
 
-        peak_of_head = held.tile([P, H], F32, name="peak_of_head")
-        nc.vector.tensor_reduce(out=peak_of_head[:], in_=by_point[:], axis=X, op=ALU.max)
-        peaks_flipped = held.tile([P, H, DPH], F32, name="peaks_flipped")
-        nc.vector.tensor_copy(peaks_flipped[:], peak_of_head[:].unsqueeze(2).to_broadcast([P, H, DPH]))
-        peaks = psum_held.tile([D, P], F32, name="peaks")
-        nc.tensor.transpose(peaks[:], peaks_flipped[:].rearrange("p h r -> p (h r)"), identity[:])
-
         terms = [held.tile([D, T + 1, PTS, NB], F32, name=f"terms{k}") for k in range(PIECES)]
         sums = [None] * PIECES
         projected = [None] * PIECES
 
         def weigh(k):
+            peak = work.tile([D, PTS], F32, name="peak")
+            nc.vector.tensor_reduce(out=peak[:], in_=logits[k][:], axis=X, op=ALU.max)
             shifted = work.tile([D, PTS, NB], F32, name="shifted")
             nc.vector.tensor_tensor(
-                shifted[:],
-                logits[k][:],
-                peaks[:, k * PTS : (k + 1) * PTS].unsqueeze(2).to_broadcast([D, PTS, NB]),
-                ALU.subtract,
+                shifted[:], logits[k][:], peak[:].unsqueeze(2).to_broadcast([D, PTS, NB]), ALU.subtract
             )
             nc.scalar.activation(terms[k][:, T], shifted[:], EXP, scale=0.25)
 

@@ -11,6 +11,8 @@ T = 3
 S = 512
 P = 128
 NB = 16
+H = 8
+DPH = D // H
 N = P * NB
 PIECE = 512
 PIECES = N // PIECE
@@ -26,23 +28,26 @@ def tile_transformerdecoderlayer_equi_v4_kernel(tc, v, dist, wo, tgt, offs, out)
         tc.tile_pool(name="held", bufs=1) as held,
         tc.tile_pool(name="work", bufs=2) as work,
         tc.psum_pool(name="psum", bufs=2) as psum,
+        tc.psum_pool(name="psum_held", bufs=1) as psum_held,
     ):
-        offsets = held.tile([D, N // 16], U16, name="offsets")
-        nc.sync.dma_start(offsets[:], offs)
+        by_point = held.tile([P, H, NB], F32, name="by_point")
+        nc.sync.dma_start(by_point[:], dist.rearrange("(h r) (p n) -> r p h n", r=DPH, n=NB)[0])
         logits = [held.tile([D, PTS, NB], F32, name=f"logits{k}") for k in range(PIECES)]
         values = [held.tile([D, S], F32, name=f"values{t}") for t in range(T)]
         pieces_of_dist = dist.rearrange("d (k p n) -> k d p n", p=PTS, n=NB)
         nc.scalar.dma_start(logits[0][:], pieces_of_dist[0])
-        nc.sync.dma_start(logits[1][:], pieces_of_dist[1])
+        offsets = held.tile([D, N // 16], U16, name="offsets")
+        nc.sync.dma_start(offsets[:], offs)
         nc.scalar.dma_start(values[0][:], v[0:D, :])
-        nc.sync.dma_start(values[1][:], v[D : 2 * D, :])
-        nc.scalar.dma_start(values[2][:], v[2 * D : 3 * D, :])
-        nc.sync.dma_start(logits[2][:], pieces_of_dist[2])
-        nc.scalar.dma_start(logits[3][:], pieces_of_dist[3])
+        nc.sync.dma_start(logits[1][:], pieces_of_dist[1])
+        nc.scalar.dma_start(values[1][:], v[D : 2 * D, :])
+        nc.sync.dma_start(values[2][:], v[2 * D : 3 * D, :])
+        nc.scalar.dma_start(logits[2][:], pieces_of_dist[2])
+        nc.sync.dma_start(logits[3][:], pieces_of_dist[3])
         weights = held.tile([D, D], BF16, name="weights")
-        nc.sync.dma_start(weights[:], wo)
+        nc.scalar.dma_start(weights[:], wo)
         own = held.tile([D, T, P], F32, name="own")
-        nc.scalar.dma_start(own[:], tgt.rearrange("(t o) p -> o t p", o=D))
+        nc.sync.dma_start(own[:], tgt.rearrange("(t o) p -> o t p", o=D))
 
         identity = held.tile([D, D], F32, name="identity")
         make_identity(nc, identity[:])
@@ -52,18 +57,33 @@ def tile_transformerdecoderlayer_equi_v4_kernel(tc, v, dist, wo, tgt, offs, out)
         one = held.tile([D, 1], F32, name="one")
         nc.scalar.activation(one[:], zero[:], EXP)
 
+        peak_of_head = held.tile([P, H], F32, name="peak_of_head")
+        nc.vector.tensor_reduce(out=peak_of_head[:], in_=by_point[:], axis=X, op=ALU.max)
+        peaks_flipped = held.tile([P, H, DPH], F32, name="peaks_flipped")
+        nc.vector.tensor_copy(peaks_flipped[:], peak_of_head[:].unsqueeze(2).to_broadcast([P, H, DPH]))
+        peaks = psum_held.tile([D, P], F32, name="peaks")
+        nc.tensor.transpose(peaks[:], peaks_flipped[:].rearrange("p h r -> p (h r)"), identity[:])
+
         terms = [held.tile([D, T + 1, PTS, NB], F32, name=f"terms{k}") for k in range(PIECES)]
         sums = [None] * PIECES
         projected = [None] * PIECES
 
-        def weigh(k):
-            peak = work.tile([D, PTS], F32, name="peak")
-            nc.vector.tensor_reduce(out=peak[:], in_=logits[k][:], axis=X, op=ALU.max)
-            shifted = work.tile([D, PTS, NB], F32, name="shifted")
+        bias = held.tile([D, P], F32, name="bias")
+
+        def weigh_first():
+            shifted = held.tile([D, PTS, NB], F32, name="shifted")
             nc.vector.tensor_tensor(
-                shifted[:], logits[k][:], peak[:].unsqueeze(2).to_broadcast([D, PTS, NB]), ALU.subtract
+                shifted[:], logits[0][:], peaks[:, 0:PTS].unsqueeze(2).to_broadcast([D, PTS, NB]), ALU.subtract
             )
-            nc.scalar.activation(terms[k][:, T], shifted[:], EXP, scale=0.25)
+            nc.scalar.activation(terms[0][:, T], shifted[:], EXP, scale=0.25)
+            nc.vector.tensor_scalar_mul(bias[:], peaks[:], -0.25)
+
+        def weigh(k):
+            for p in range(PTS):
+                point = k * PTS + p
+                nc.scalar.activation(
+                    terms[k][:, T, p, :], logits[k][:, p, :], EXP, bias=bias[:, point : point + 1], scale=0.25
+                )
 
         def look_up(k, t):
             nc.vector.tensor_tensor(
@@ -107,7 +127,7 @@ def tile_transformerdecoderlayer_equi_v4_kernel(tc, v, dist, wo, tgt, offs, out)
             nc.vector.tensor_tensor(result[:], projected[k][:], own[:, :, points], ALU.add)
             nc.sync.dma_start(out.rearrange("(t o) p -> o t p", o=D)[:, :, points], result[:])
 
-        weigh(0)
+        weigh_first()
         weigh(1)
         for k in range(PIECES):
             look_up(k, 0)

@@ -59,16 +59,17 @@ def tile_transformerdecoderlayer_equi_v4_kernel(tc, v, dist, wo, tgt, offs, out)
 
         peak_of_head = held.tile([P, H], F32, name="peak_of_head")
         nc.vector.tensor_reduce(out=peak_of_head[:], in_=by_point[:], axis=X, op=ALU.max)
+        stats = psum_held.tile([D, 2, P], F32, name="stats")
+        peaks = stats[:, 0, :]
         peaks_flipped = held.tile([P, H, DPH], F32, name="peaks_flipped")
         nc.vector.tensor_copy(peaks_flipped[:], peak_of_head[:].unsqueeze(2).to_broadcast([P, H, DPH]))
-        peaks = psum_held.tile([D, P], F32, name="peaks")
-        nc.tensor.transpose(peaks[:], peaks_flipped[:].rearrange("p h r -> p (h r)"), identity[:])
+        nc.tensor.transpose(peaks, peaks_flipped[:].rearrange("p h r -> p (h r)"), identity[:])
 
         terms = [held.tile([D, T + 1, PTS, NB], F32, name=f"terms{k}") for k in range(PIECES)]
         sums = [None] * PIECES
-        projected = [None] * PIECES
 
         bias = held.tile([D, P], F32, name="bias")
+        inverse = held.tile([D, P], F32, name="inverse")
 
         def weigh_first():
             shifted = held.tile([D, PTS, NB], F32, name="shifted")
@@ -76,7 +77,7 @@ def tile_transformerdecoderlayer_equi_v4_kernel(tc, v, dist, wo, tgt, offs, out)
                 shifted[:], logits[0][:], peaks[:, 0:PTS].unsqueeze(2).to_broadcast([D, PTS, NB]), ALU.subtract
             )
             nc.scalar.activation(terms[0][:, T], shifted[:], EXP, scale=0.25)
-            nc.vector.tensor_scalar_mul(bias[:], peaks[:], -0.25)
+            nc.vector.tensor_scalar_mul(bias[:], peaks, -0.25)
 
         def weigh(k):
             for p in range(PTS):
@@ -84,6 +85,32 @@ def tile_transformerdecoderlayer_equi_v4_kernel(tc, v, dist, wo, tgt, offs, out)
                 nc.scalar.activation(
                     terms[k][:, T, p, :], logits[k][:, p, :], EXP, bias=bias[:, point : point + 1], scale=0.25
                 )
+
+        total_of_head = held.tile([P, H], F32, name="total_of_head")
+        inverse_of_head = held.tile([P, H], F32, name="inverse_of_head")
+
+        def add_up_weights():
+            bias_of_head = held.tile([P, H], F32, name="bias_of_head")
+            nc.vector.tensor_scalar_mul(bias_of_head[:], peak_of_head[:], -0.25)
+            weight_by_point = held.tile([P, H, NB], F32, name="weight_by_point")
+            for h in range(H):
+                nc.scalar.activation(
+                    weight_by_point[:, h, :],
+                    by_point[:, h, :],
+                    EXP,
+                    bias=bias_of_head[:, h : h + 1],
+                    scale=0.25,
+                    accum_out=total_of_head[:, h : h + 1],
+                )
+
+        def invert_totals():
+            nc.vector.reciprocal(inverse_of_head[:], total_of_head[:])
+
+        def spread_inverses():
+            inverse_flipped = held.tile([P, H, DPH], F32, name="inverse_flipped")
+            nc.vector.tensor_copy(inverse_flipped[:], inverse_of_head[:].unsqueeze(2).to_broadcast([P, H, DPH]))
+            nc.tensor.transpose(stats[:, 1, :], inverse_flipped[:].rearrange("p h r -> p (h r)"), identity[:])
+            nc.scalar.copy(inverse[:], stats[:, 1, :])
 
         def look_up(k, t):
             nc.vector.tensor_tensor(
@@ -94,55 +121,62 @@ def tile_transformerdecoderlayer_equi_v4_kernel(tc, v, dist, wo, tgt, offs, out)
             )
 
         def sum_on_tensor(k):
-            by_neighbour = terms[k][:].rearrange("d t p n -> d (t p) n")
-            flipped = psum.tile([(T + 1) * PTS, D], F32, name="flipped")
+            by_neighbour = terms[k][:, 0:T].rearrange("d t p n -> d (t p) n")
+            flipped = psum.tile([T * PTS, D], F32, name="flipped")
             for n in range(NB):
                 nc.tensor.matmul(
                     flipped[:], by_neighbour[:, :, n], identity[:], is_transpose=True, start=(n == 0), stop=(n == NB - 1)
                 )
-            flipped_sb = work.tile([(T + 1) * PTS, D], F32, name="flipped_sb")
+            flipped_sb = work.tile([T * PTS, D], F32, name="flipped_sb")
             nc.scalar.copy(flipped_sb[:], flipped[:])
-            sums[k] = psum.tile([D, T + 1, PTS], F32, name="sums")
-            nc.tensor.transpose(sums[k][:].rearrange("d t p -> d (t p)"), flipped_sb[:], identity[:])
+            sums[k] = psum.tile([D, T, PTS], F32, name="sums")
+            nc.tensor.transpose(sums[k][:].rearrange("d t p -> d (t p)"), flipped_sb[:], identity[0 : T * PTS, 0 : T * PTS])
 
         def sum_on_vector(k):
-            sums[k] = work.tile([D, T + 1, PTS], F32, name="sums_sb")
-            nc.vector.tensor_reduce(out=sums[k][:], in_=terms[k][:], axis=X, op=ALU.add)
+            sums[k] = work.tile([D, T, PTS], F32, name="sums_sb")
+            nc.vector.tensor_reduce(out=sums[k][:], in_=terms[k][:, 0:T], axis=X, op=ALU.add)
 
-        def divide_and_project(k):
-            inverse = work.tile([D, PTS], F32, name="inverse")
-            nc.vector.reciprocal(inverse[:], sums[k][:, T])
-            agg = work.tile([D, T, PTS], BF16, name="agg")
-            nc.vector.tensor_tensor(
-                agg[:], sums[k][:, 0:T], inverse[:].unsqueeze(1).to_broadcast([D, T, PTS]), ALU.mult
-            )
-            projected[k] = psum.tile([D, T, PTS], F32, name="projected")
+        projected = [None] * PIECES
+
+        def divide_and_project(first):
+            agg = work.tile([D, T, 2, PTS], BF16, name="agg")
+            for g in range(2):
+                k = first + g
+                nc.vector.tensor_tensor(
+                    agg[:, :, g, :],
+                    sums[k][:],
+                    inverse[:, k * PTS : (k + 1) * PTS].unsqueeze(1).to_broadcast([D, T, PTS]),
+                    ALU.mult,
+                )
+            projected[first] = psum.tile([D, T, 2 * PTS], F32, name="projected")
             nc.tensor.matmul(
-                projected[k][:].rearrange("o t p -> o (t p)"), weights[:], agg[:].rearrange("d t p -> d (t p)")
+                projected[first][:].rearrange("o t p -> o (t p)"), weights[:], agg[:].rearrange("d t g p -> d (t g p)")
             )
 
-        def add_own_and_store(k):
-            points = slice(k * PTS, (k + 1) * PTS)
-            result = work.tile([D, T, PTS], F32, name="result")
-            nc.vector.tensor_tensor(result[:], projected[k][:], own[:, :, points], ALU.add)
+        def add_own_and_store(first):
+            points = slice(first * PTS, (first + 2) * PTS)
+            result = work.tile([D, T, 2 * PTS], F32, name="result")
+            nc.vector.tensor_tensor(result[:], projected[first][:], own[:, :, points], ALU.add)
             nc.sync.dma_start(out.rearrange("(t o) p -> o t p", o=D)[:, :, points], result[:])
 
         weigh_first()
-        weigh(1)
+        for k in range(1, PIECES):
+            weigh(k)
+        add_up_weights()
         for k in range(PIECES):
             look_up(k, 0)
-            if k >= 2:
-                divide_and_project(k - 2)
+            if k == 1:
+                invert_totals()
+            if k == 3:
+                divide_and_project(0)
             look_up(k, 1)
-            if k >= 2:
-                add_own_and_store(k - 2)
+            if k == 1:
+                spread_inverses()
+            if k == 3:
+                add_own_and_store(0)
             look_up(k, 2)
             if k < PIECES - 1:
                 sum_on_tensor(k)
-            if k + 2 < PIECES:
-                weigh(k + 2)
         sum_on_vector(PIECES - 1)
-        divide_and_project(PIECES - 2)
-        divide_and_project(PIECES - 1)
-        add_own_and_store(PIECES - 2)
-        add_own_and_store(PIECES - 1)
+        divide_and_project(2)
+        add_own_and_store(2)

@@ -26,28 +26,28 @@ def tile_transformerdecoderlayer_equi_v4_kernel(tc, v, dist, wo, tgt, offs, out)
     nc = tc.nc
     with (
         tc.tile_pool(name="held", bufs=1) as held,
+        tc.tile_pool(name="scratch", bufs=1) as scratch,
         tc.tile_pool(name="work", bufs=2) as work,
         tc.psum_pool(name="psum", bufs=2) as psum,
         tc.psum_pool(name="psum_held", bufs=1) as psum_held,
     ):
-        by_point = held.tile([P, H, NB], F32, name="by_point")
-        nc.sync.dma_start(by_point[:], dist.rearrange("(h r) (p n) -> r p h n", r=DPH, n=NB)[0])
         logits = [held.tile([D, PTS, NB], F32, name=f"logits{k}") for k in range(PIECES)]
         values = [held.tile([D, S], F32, name=f"values{t}") for t in range(T)]
         pieces_of_dist = dist.rearrange("d (k p n) -> k d p n", p=PTS, n=NB)
-        nc.scalar.dma_start(logits[0][:], pieces_of_dist[0])
+        nc.sync.dma_start(logits[0][:], pieces_of_dist[0])
+        by_point = held.tile([P, H, NB], F32, name="by_point")
+        nc.scalar.dma_start(by_point[:], dist.rearrange("(h r) (p n) -> r p h n", r=DPH, n=NB)[0])
         offsets = held.tile([D, N // 16], U16, name="offsets")
         nc.sync.dma_start(offsets[:], offs)
         nc.scalar.dma_start(values[0][:], v[0:D, :])
-        nc.sync.dma_start(logits[1][:], pieces_of_dist[1])
-        nc.scalar.dma_start(values[1][:], v[D : 2 * D, :])
+        nc.sync.dma_start(values[1][:], v[D : 2 * D, :])
         nc.sync.dma_start(values[2][:], v[2 * D : 3 * D, :])
-        nc.scalar.dma_start(logits[2][:], pieces_of_dist[2])
-        nc.sync.dma_start(logits[3][:], pieces_of_dist[3])
-        weights = held.tile([D, D], BF16, name="weights")
-        nc.scalar.dma_start(weights[:], wo)
+        for k in range(1, PIECES):
+            nc.sync.dma_start(logits[k][:], pieces_of_dist[k])
         own = held.tile([D, T, P], F32, name="own")
         nc.sync.dma_start(own[:], tgt.rearrange("(t o) p -> o t p", o=D))
+        weights = held.tile([D, D], BF16, name="weights")
+        nc.sync.dma_start(weights[:], wo)
 
         identity = held.tile([D, D], F32, name="identity")
         make_identity(nc, identity[:])
@@ -57,27 +57,33 @@ def tile_transformerdecoderlayer_equi_v4_kernel(tc, v, dist, wo, tgt, offs, out)
         one = held.tile([D, 1], F32, name="one")
         nc.scalar.activation(one[:], zero[:], EXP)
 
+        terms = [held.tile([D, T + 1, PTS, NB], F32, name=f"terms{k}") for k in range(PIECES)]
+        sums = [None] * PIECES
+        projected = [None] * PIECES
+
+        halves = [slice(0, PTS // 2), slice(PTS // 2, PTS)]
+        first_peaks = held.tile([D, PTS], F32, name="first_peaks")
+        shifted = scratch.tile([D, PTS, NB], F32, tag="scratch", name="shifted")
+        for half in halves:
+            nc.vector.tensor_reduce(out=first_peaks[:, half], in_=logits[0][:, half, :], axis=X, op=ALU.max)
+        for half in halves:
+            nc.vector.tensor_tensor(
+                shifted[:, half, :],
+                logits[0][:, half, :],
+                first_peaks[:, half].unsqueeze(2).to_broadcast([D, PTS // 2, NB]),
+                ALU.subtract,
+            )
+            nc.scalar.activation(terms[0][:, T, half, :], shifted[:, half, :], EXP, scale=0.25)
+
         peak_of_head = held.tile([P, H], F32, name="peak_of_head")
         nc.vector.tensor_reduce(out=peak_of_head[:], in_=by_point[:], axis=X, op=ALU.max)
         stats = psum_held.tile([D, 2, P], F32, name="stats")
-        peaks = stats[:, 0, :]
-        peaks_flipped = held.tile([P, H, DPH], F32, name="peaks_flipped")
-        nc.vector.tensor_copy(peaks_flipped[:], peak_of_head[:].unsqueeze(2).to_broadcast([P, H, DPH]))
-        nc.tensor.transpose(peaks, peaks_flipped[:].rearrange("p h r -> p (h r)"), identity[:])
-
-        terms = [held.tile([D, T + 1, PTS, NB], F32, name=f"terms{k}") for k in range(PIECES)]
-        sums = [None] * PIECES
-
+        bias_flipped = held.tile([P, H, DPH], F32, name="bias_flipped")
+        nc.vector.tensor_scalar_mul(bias_flipped[:], peak_of_head[:].unsqueeze(2).to_broadcast([P, H, DPH]), -0.25)
+        nc.tensor.transpose(stats[:, 0, :], bias_flipped[:].rearrange("p h r -> p (h r)"), identity[:])
         bias = held.tile([D, P], F32, name="bias")
+        nc.scalar.copy(bias[:], stats[:, 0, :])
         inverse = held.tile([D, P], F32, name="inverse")
-
-        def weigh_first():
-            shifted = held.tile([D, PTS, NB], F32, name="shifted")
-            nc.vector.tensor_tensor(
-                shifted[:], logits[0][:], peaks[:, 0:PTS].unsqueeze(2).to_broadcast([D, PTS, NB]), ALU.subtract
-            )
-            nc.scalar.activation(terms[0][:, T], shifted[:], EXP, scale=0.25)
-            nc.vector.tensor_scalar_mul(bias[:], peaks, -0.25)
 
         def weigh(k):
             for p in range(PTS):
@@ -90,15 +96,13 @@ def tile_transformerdecoderlayer_equi_v4_kernel(tc, v, dist, wo, tgt, offs, out)
         inverse_of_head = held.tile([P, H], F32, name="inverse_of_head")
 
         def add_up_weights():
-            bias_of_head = held.tile([P, H], F32, name="bias_of_head")
-            nc.vector.tensor_scalar_mul(bias_of_head[:], peak_of_head[:], -0.25)
-            weight_by_point = held.tile([P, H, NB], F32, name="weight_by_point")
+            weight_by_point = scratch.tile([P, H, NB], F32, tag="scratch", name="weight_by_point")
             for h in range(H):
                 nc.scalar.activation(
                     weight_by_point[:, h, :],
                     by_point[:, h, :],
                     EXP,
-                    bias=bias_of_head[:, h : h + 1],
+                    bias=bias_flipped[:, h, 0:1],
                     scale=0.25,
                     accum_out=total_of_head[:, h : h + 1],
                 )
@@ -112,11 +116,11 @@ def tile_transformerdecoderlayer_equi_v4_kernel(tc, v, dist, wo, tgt, offs, out)
             nc.tensor.transpose(stats[:, 1, :], inverse_flipped[:].rearrange("p h r -> p (h r)"), identity[:])
             nc.scalar.copy(inverse[:], stats[:, 1, :])
 
-        def look_up(k, t):
+        def look_up(k, t, points):
             nc.vector.tensor_tensor(
-                terms[k][:, t].rearrange("d p n -> d (p n)"),
-                values[t][:].indirect(offsets[:, k * COLS : (k + 1) * COLS]),
-                terms[k][:, T].rearrange("d p n -> d (p n)"),
+                terms[k][:, t, points, :].rearrange("d p n -> d (p n)"),
+                values[t][:].indirect(offsets[:, k * PTS + points.start : k * PTS + points.stop]),
+                terms[k][:, T, points, :].rearrange("d p n -> d (p n)"),
                 ALU.mult,
             )
 
@@ -135,8 +139,6 @@ def tile_transformerdecoderlayer_equi_v4_kernel(tc, v, dist, wo, tgt, offs, out)
         def sum_on_vector(k):
             sums[k] = work.tile([D, T, PTS], F32, name="sums_sb")
             nc.vector.tensor_reduce(out=sums[k][:], in_=terms[k][:, 0:T], axis=X, op=ALU.add)
-
-        projected = [None] * PIECES
 
         def divide_and_project(first):
             agg = work.tile([D, T, 2, PTS], BF16, name="agg")
@@ -159,22 +161,26 @@ def tile_transformerdecoderlayer_equi_v4_kernel(tc, v, dist, wo, tgt, offs, out)
             nc.vector.tensor_tensor(result[:], projected[first][:], own[:, :, points], ALU.add)
             nc.sync.dma_start(out.rearrange("(t o) p -> o t p", o=D)[:, :, points], result[:])
 
-        weigh_first()
+        whole = slice(0, PTS)
         for k in range(1, PIECES):
             weigh(k)
         add_up_weights()
-        for k in range(PIECES):
-            look_up(k, 0)
+        for half in halves:
+            for t in range(T):
+                look_up(0, t, half)
+        sum_on_tensor(0)
+        for k in range(1, PIECES):
+            look_up(k, 0, whole)
             if k == 1:
                 invert_totals()
             if k == 3:
                 divide_and_project(0)
-            look_up(k, 1)
+            look_up(k, 1, whole)
             if k == 1:
                 spread_inverses()
             if k == 3:
                 add_own_and_store(0)
-            look_up(k, 2)
+            look_up(k, 2, whole)
             if k < PIECES - 1:
                 sum_on_tensor(k)
         sum_on_vector(PIECES - 1)

@@ -17,6 +17,7 @@ N = P * NB
 PIECE = 512
 PIECES = N // PIECE
 PTS = PIECE // NB
+FIRST = 8
 COLS = PIECE // 16
 
 FLOPS = 2 * T * D * N + 2 * D * D * T * P
@@ -34,7 +35,8 @@ def tile_transformerdecoderlayer_equi_v4_kernel(tc, v, dist, wo, tgt, offs, out)
         logits = [held.tile([D, PTS, NB], F32, name=f"logits{k}") for k in range(PIECES)]
         values = [held.tile([D, S], F32, name=f"values{t}") for t in range(T)]
         pieces_of_dist = dist.rearrange("d (k p n) -> k d p n", p=PTS, n=NB)
-        nc.sync.dma_start(logits[0][:], pieces_of_dist[0])
+        nc.sync.dma_start(logits[0][:, 0:FIRST, :], pieces_of_dist[0][:, 0:FIRST, :])
+        nc.sync.dma_start(logits[0][:, FIRST:PTS, :], pieces_of_dist[0][:, FIRST:PTS, :])
         by_point = held.tile([P, H, NB], F32, name="by_point")
         nc.scalar.dma_start(by_point[:], dist.rearrange("(h r) (p n) -> r p h n", r=DPH, n=NB)[0])
         offsets = held.tile([D, N // 16], U16, name="offsets")
@@ -61,7 +63,7 @@ def tile_transformerdecoderlayer_equi_v4_kernel(tc, v, dist, wo, tgt, offs, out)
         sums = [None] * PIECES
         projected = [None] * PIECES
 
-        halves = [slice(0, PTS // 2), slice(PTS // 2, PTS)]
+        halves = [slice(0, FIRST), slice(FIRST, 2 * FIRST), slice(2 * FIRST, PTS)]
         first_peaks = held.tile([D, PTS], F32, name="first_peaks")
         shifted = scratch.tile([D, PTS, NB], F32, tag="scratch", name="shifted")
         for half in halves:
@@ -70,7 +72,7 @@ def tile_transformerdecoderlayer_equi_v4_kernel(tc, v, dist, wo, tgt, offs, out)
             nc.vector.tensor_tensor(
                 shifted[:, half, :],
                 logits[0][:, half, :],
-                first_peaks[:, half].unsqueeze(2).to_broadcast([D, PTS // 2, NB]),
+                first_peaks[:, half].unsqueeze(2).to_broadcast([D, half.stop - half.start, NB]),
                 ALU.subtract,
             )
             nc.scalar.activation(terms[0][:, T, half, :], shifted[:, half, :], EXP, scale=0.25)

@@ -14,11 +14,10 @@ NB = 16
 H = 8
 DPH = D // H
 N = P * NB
-PIECE = 512
-PIECES = N // PIECE
-PTS = PIECE // NB
-FIRST = 8
-COLS = PIECE // 16
+SIZES = [32, 32, 32, 32]
+STARTS = [sum(SIZES[:k]) for k in range(len(SIZES))]
+PIECES = len(SIZES)
+PARTS = [slice(0, 8), slice(8, 16), slice(16, 32)]
 
 FLOPS = 2 * T * D * N + 2 * D * D * T * P
 
@@ -32,11 +31,12 @@ def tile_transformerdecoderlayer_equi_v4_kernel(tc, v, dist, wo, tgt, offs, out)
         tc.psum_pool(name="psum", bufs=2) as psum,
         tc.psum_pool(name="psum_held", bufs=1) as psum_held,
     ):
-        logits = [held.tile([D, PTS, NB], F32, name=f"logits{k}") for k in range(PIECES)]
+        logits = [held.tile([D, SIZES[k], NB], F32, name=f"logits{k}") for k in range(PIECES)]
         values = [held.tile([D, S], F32, name=f"values{t}") for t in range(T)]
-        pieces_of_dist = dist.rearrange("d (k p n) -> k d p n", p=PTS, n=NB)
-        nc.sync.dma_start(logits[0][:, 0:FIRST, :], pieces_of_dist[0][:, 0:FIRST, :])
-        nc.sync.dma_start(logits[0][:, FIRST:PTS, :], pieces_of_dist[0][:, FIRST:PTS, :])
+        by_entry = dist.rearrange("d (p n) -> d p n", n=NB)
+        first = PARTS[0].stop
+        nc.sync.dma_start(logits[0][:, 0:first, :], by_entry[:, 0:first, :])
+        nc.sync.dma_start(logits[0][:, first : SIZES[0], :], by_entry[:, first : SIZES[0], :])
         by_point = held.tile([P, H, NB], F32, name="by_point")
         nc.scalar.dma_start(by_point[:], dist.rearrange("(h r) (p n) -> r p h n", r=DPH, n=NB)[0])
         offsets = held.tile([D, N // 16], U16, name="offsets")
@@ -45,7 +45,7 @@ def tile_transformerdecoderlayer_equi_v4_kernel(tc, v, dist, wo, tgt, offs, out)
         nc.sync.dma_start(values[1][:], v[D : 2 * D, :])
         nc.sync.dma_start(values[2][:], v[2 * D : 3 * D, :])
         for k in range(1, PIECES):
-            nc.sync.dma_start(logits[k][:], pieces_of_dist[k])
+            nc.sync.dma_start(logits[k][:], by_entry[:, STARTS[k] : STARTS[k] + SIZES[k], :])
         own = held.tile([D, T, P], F32, name="own")
         nc.sync.dma_start(own[:], tgt.rearrange("(t o) p -> o t p", o=D))
         weights = held.tile([D, D], BF16, name="weights")
@@ -59,23 +59,22 @@ def tile_transformerdecoderlayer_equi_v4_kernel(tc, v, dist, wo, tgt, offs, out)
         one = held.tile([D, 1], F32, name="one")
         nc.scalar.activation(one[:], zero[:], EXP)
 
-        terms = [held.tile([D, T + 1, PTS, NB], F32, name=f"terms{k}") for k in range(PIECES)]
+        terms = [held.tile([D, T + 1, SIZES[k], NB], F32, name=f"terms{k}") for k in range(PIECES)]
         sums = [None] * PIECES
         projected = [None] * PIECES
 
-        halves = [slice(0, FIRST), slice(FIRST, 2 * FIRST), slice(2 * FIRST, PTS)]
-        first_peaks = held.tile([D, PTS], F32, name="first_peaks")
-        shifted = scratch.tile([D, PTS, NB], F32, tag="scratch", name="shifted")
-        for half in halves:
-            nc.vector.tensor_reduce(out=first_peaks[:, half], in_=logits[0][:, half, :], axis=X, op=ALU.max)
-        for half in halves:
+        first_peaks = held.tile([D, SIZES[0]], F32, name="first_peaks")
+        shifted = scratch.tile([D, SIZES[0], NB], F32, tag="scratch", name="shifted")
+        for part in PARTS:
+            nc.vector.tensor_reduce(out=first_peaks[:, part], in_=logits[0][:, part, :], axis=X, op=ALU.max)
+        for part in PARTS:
             nc.vector.tensor_tensor(
-                shifted[:, half, :],
-                logits[0][:, half, :],
-                first_peaks[:, half].unsqueeze(2).to_broadcast([D, half.stop - half.start, NB]),
+                shifted[:, part, :],
+                logits[0][:, part, :],
+                first_peaks[:, part].unsqueeze(2).to_broadcast([D, part.stop - part.start, NB]),
                 ALU.subtract,
             )
-            nc.scalar.activation(terms[0][:, T, half, :], shifted[:, half, :], EXP, scale=0.25)
+            nc.scalar.activation(terms[0][:, T, part, :], shifted[:, part, :], EXP, scale=0.25)
 
         peak_of_head = held.tile([P, H], F32, name="peak_of_head")
         nc.vector.tensor_reduce(out=peak_of_head[:], in_=by_point[:], axis=X, op=ALU.max)
@@ -88,31 +87,23 @@ def tile_transformerdecoderlayer_equi_v4_kernel(tc, v, dist, wo, tgt, offs, out)
         inverse = held.tile([D, P], F32, name="inverse")
 
         def weigh(k):
-            for p in range(PTS):
-                point = k * PTS + p
+            for p in range(SIZES[k]):
+                point = STARTS[k] + p
                 nc.scalar.activation(
                     terms[k][:, T, p, :], logits[k][:, p, :], EXP, bias=bias[:, point : point + 1], scale=0.25
                 )
 
-        total_of_head = held.tile([P, H], F32, name="total_of_head")
-        inverse_of_head = held.tile([P, H], F32, name="inverse_of_head")
-
-        def add_up_weights():
-            weight_by_point = scratch.tile([P, H, NB], F32, tag="scratch", name="weight_by_point")
-            for h in range(H):
-                nc.scalar.activation(
-                    weight_by_point[:, h, :],
-                    by_point[:, h, :],
-                    EXP,
-                    bias=bias_flipped[:, h, 0:1],
-                    scale=0.25,
-                    accum_out=total_of_head[:, h : h + 1],
-                )
-
         def invert_totals():
+            shifted_by_point = held.tile([P, H, NB], F32, name="shifted_by_point")
+            nc.vector.tensor_tensor(
+                shifted_by_point[:], by_point[:], peak_of_head[:].unsqueeze(2).to_broadcast([P, H, NB]), ALU.subtract
+            )
+            weight_by_point = scratch.tile([P, H, NB], F32, tag="scratch", name="weight_by_point")
+            nc.scalar.activation(weight_by_point[:], shifted_by_point[:], EXP, scale=0.25)
+            total_of_head = held.tile([P, H], F32, name="total_of_head")
+            nc.vector.tensor_reduce(out=total_of_head[:], in_=weight_by_point[:], axis=X, op=ALU.add)
+            inverse_of_head = held.tile([P, H], F32, name="inverse_of_head")
             nc.vector.reciprocal(inverse_of_head[:], total_of_head[:])
-
-        def spread_inverses():
             inverse_flipped = held.tile([P, H, DPH], F32, name="inverse_flipped")
             nc.vector.tensor_copy(inverse_flipped[:], inverse_of_head[:].unsqueeze(2).to_broadcast([P, H, DPH]))
             nc.tensor.transpose(stats[:, 1, :], inverse_flipped[:].rearrange("p h r -> p (h r)"), identity[:])
@@ -121,70 +112,65 @@ def tile_transformerdecoderlayer_equi_v4_kernel(tc, v, dist, wo, tgt, offs, out)
         def look_up(k, t, points):
             nc.vector.tensor_tensor(
                 terms[k][:, t, points, :].rearrange("d p n -> d (p n)"),
-                values[t][:].indirect(offsets[:, k * PTS + points.start : k * PTS + points.stop]),
+                values[t][:].indirect(offsets[:, STARTS[k] + points.start : STARTS[k] + points.stop]),
                 terms[k][:, T, points, :].rearrange("d p n -> d (p n)"),
                 ALU.mult,
             )
 
         def sum_on_tensor(k):
+            columns = T * SIZES[k]
             by_neighbour = terms[k][:, 0:T].rearrange("d t p n -> d (t p) n")
-            flipped = psum.tile([T * PTS, D], F32, name="flipped")
+            flipped = psum.tile([columns, D], F32, name="flipped")
             for n in range(NB):
                 nc.tensor.matmul(
                     flipped[:], by_neighbour[:, :, n], identity[:], is_transpose=True, start=(n == 0), stop=(n == NB - 1)
                 )
-            flipped_sb = work.tile([T * PTS, D], F32, name="flipped_sb")
+            flipped_sb = work.tile([columns, D], F32, name="flipped_sb")
             nc.scalar.copy(flipped_sb[:], flipped[:])
-            sums[k] = psum.tile([D, T, PTS], F32, name="sums")
-            nc.tensor.transpose(sums[k][:].rearrange("d t p -> d (t p)"), flipped_sb[:], identity[0 : T * PTS, 0 : T * PTS])
+            sums[k] = psum.tile([D, T, SIZES[k]], F32, name="sums")
+            nc.tensor.transpose(sums[k][:].rearrange("d t p -> d (t p)"), flipped_sb[:], identity[0:columns, 0:columns])
 
         def sum_on_vector(k):
-            sums[k] = work.tile([D, T, PTS], F32, name="sums_sb")
+            sums[k] = work.tile([D, T, SIZES[k]], F32, name="sums_sb")
             nc.vector.tensor_reduce(out=sums[k][:], in_=terms[k][:, 0:T], axis=X, op=ALU.add)
 
-        def divide_and_project(first):
-            agg = work.tile([D, T, 2, PTS], BF16, name="agg")
-            for g in range(2):
-                k = first + g
+        def divide_and_project(first_piece):
+            points = SIZES[first_piece] + SIZES[first_piece + 1]
+            agg = work.tile([D, T, points], BF16, name="agg")
+            for k in (first_piece, first_piece + 1):
+                begin = STARTS[k] - STARTS[first_piece]
                 nc.vector.tensor_tensor(
-                    agg[:, :, g, :],
+                    agg[:, :, begin : begin + SIZES[k]],
                     sums[k][:],
-                    inverse[:, k * PTS : (k + 1) * PTS].unsqueeze(1).to_broadcast([D, T, PTS]),
+                    inverse[:, STARTS[k] : STARTS[k] + SIZES[k]].unsqueeze(1).to_broadcast([D, T, SIZES[k]]),
                     ALU.mult,
                 )
-            projected[first] = psum.tile([D, T, 2 * PTS], F32, name="projected")
+            projected[first_piece] = psum.tile([D, T, points], F32, name="projected")
             nc.tensor.matmul(
-                projected[first][:].rearrange("o t p -> o (t p)"), weights[:], agg[:].rearrange("d t g p -> d (t g p)")
+                projected[first_piece][:].rearrange("o t p -> o (t p)"), weights[:], agg[:].rearrange("d t p -> d (t p)")
             )
 
-        def add_own_and_store(first):
-            points = slice(first * PTS, (first + 2) * PTS)
-            result = work.tile([D, T, 2 * PTS], F32, name="result")
-            nc.vector.tensor_tensor(result[:], projected[first][:], own[:, :, points], ALU.add)
+        def add_own_and_store(first_piece):
+            points = slice(STARTS[first_piece], STARTS[first_piece + 1] + SIZES[first_piece + 1])
+            result = work.tile([D, T, points.stop - points.start], F32, name="result")
+            nc.vector.tensor_tensor(result[:], projected[first_piece][:], own[:, :, points], ALU.add)
             nc.sync.dma_start(out.rearrange("(t o) p -> o t p", o=D)[:, :, points], result[:])
 
-        whole = slice(0, PTS)
         for k in range(1, PIECES):
             weigh(k)
-        add_up_weights()
-        for half in halves:
+        invert_totals()
+        for part in PARTS:
             for t in range(T):
-                look_up(0, t, half)
+                look_up(0, t, part)
         sum_on_tensor(0)
         for k in range(1, PIECES):
-            look_up(k, 0, whole)
-            if k == 1:
-                invert_totals()
-            if k == 3:
-                divide_and_project(0)
-            look_up(k, 1, whole)
-            if k == 1:
-                spread_inverses()
-            if k == 3:
-                add_own_and_store(0)
-            look_up(k, 2, whole)
+            for t in range(T):
+                look_up(k, t, slice(0, SIZES[k]))
             if k < PIECES - 1:
                 sum_on_tensor(k)
+            if k == 2:
+                divide_and_project(0)
+                add_own_and_store(0)
         sum_on_vector(PIECES - 1)
         divide_and_project(2)
         add_own_and_store(2)

@@ -4,7 +4,7 @@ from concourse.masks import make_identity
 F32, BF16, U16 = mybir.dt.float32, mybir.dt.bfloat16, mybir.dt.uint16
 ALU = mybir.AluOpType
 X = mybir.AxisListType.X
-EXP = mybir.ActivationFunctionType.Exp
+EXP, COPY = mybir.ActivationFunctionType.Exp, mybir.ActivationFunctionType.Copy
 
 D = 128
 T = 3
@@ -14,10 +14,18 @@ NB = 16
 H = 8
 DPH = D // H
 N = P * NB
-SIZES = [32, 32, 32, 32]
+SIZES = [40, 40, 32, 16]
 STARTS = [sum(SIZES[:k]) for k in range(len(SIZES))]
 PIECES = len(SIZES)
-PARTS = [slice(0, 8), slice(8, 16), slice(16, 32)]
+LAST = PIECES - 1
+PARTS = [
+    [slice(0, 8), slice(8, 16), slice(16, 24), slice(24, 40)],
+    [slice(0, 16), slice(16, 40)],
+    [slice(0, 32)],
+    [slice(0, 16)],
+]
+DIRECT = PARTS[0][:2]
+DIRECT_POINTS = DIRECT[-1].stop
 
 FLOPS = 2 * T * D * N + 2 * D * D * T * P
 
@@ -34,15 +42,14 @@ def tile_transformerdecoderlayer_equi_v4_kernel(tc, v, dist, wo, tgt, offs, out)
         logits = [held.tile([D, SIZES[k], NB], F32, name=f"logits{k}") for k in range(PIECES)]
         values = [held.tile([D, S], F32, name=f"values{t}") for t in range(T)]
         by_entry = dist.rearrange("d (p n) -> d p n", n=NB)
-        first = PARTS[0].stop
-        nc.sync.dma_start(logits[0][:, 0:first, :], by_entry[:, 0:first, :])
-        nc.sync.dma_start(logits[0][:, first : SIZES[0], :], by_entry[:, first : SIZES[0], :])
+        nc.sync.dma_start(logits[0][:, 0:DIRECT_POINTS, :], by_entry[:, 0:DIRECT_POINTS, :])
         by_point = held.tile([P, H, NB], F32, name="by_point")
         nc.scalar.dma_start(by_point[:], dist.rearrange("(h r) (p n) -> r p h n", r=DPH, n=NB)[0])
+        nc.scalar.dma_start(values[0][:], v[0:D, :])
         offsets = held.tile([D, N // 16], U16, name="offsets")
         nc.sync.dma_start(offsets[:], offs)
-        nc.scalar.dma_start(values[0][:], v[0:D, :])
         nc.sync.dma_start(values[1][:], v[D : 2 * D, :])
+        nc.sync.dma_start(logits[0][:, DIRECT_POINTS : SIZES[0], :], by_entry[:, DIRECT_POINTS : SIZES[0], :])
         nc.sync.dma_start(values[2][:], v[2 * D : 3 * D, :])
         for k in range(1, PIECES):
             nc.sync.dma_start(logits[k][:], by_entry[:, STARTS[k] : STARTS[k] + SIZES[k], :])
@@ -61,13 +68,15 @@ def tile_transformerdecoderlayer_equi_v4_kernel(tc, v, dist, wo, tgt, offs, out)
 
         terms = [held.tile([D, T + 1, SIZES[k], NB], F32, name=f"terms{k}") for k in range(PIECES)]
         sums = [None] * PIECES
-        projected = [None] * PIECES
+        pairs = [slice(0, STARTS[2]), slice(STARTS[2], P)]
+        agg = [None] * len(pairs)
+        projected = [None] * len(pairs)
 
-        first_peaks = held.tile([D, SIZES[0]], F32, name="first_peaks")
-        shifted = scratch.tile([D, SIZES[0], NB], F32, tag="scratch", name="shifted")
-        for part in PARTS:
+        first_peaks = scratch.tile([D, DIRECT_POINTS], F32, tag="peaks", name="first_peaks")
+        shifted = scratch.tile([D, DIRECT_POINTS, NB], F32, tag="scratch", name="shifted")
+        for part in DIRECT:
             nc.vector.tensor_reduce(out=first_peaks[:, part], in_=logits[0][:, part, :], axis=X, op=ALU.max)
-        for part in PARTS:
+        for part in DIRECT:
             nc.vector.tensor_tensor(
                 shifted[:, part, :],
                 logits[0][:, part, :],
@@ -76,7 +85,7 @@ def tile_transformerdecoderlayer_equi_v4_kernel(tc, v, dist, wo, tgt, offs, out)
             )
             nc.scalar.activation(terms[0][:, T, part, :], shifted[:, part, :], EXP, scale=0.25)
 
-        peak_of_head = held.tile([P, H], F32, name="peak_of_head")
+        peak_of_head = scratch.tile([P, H], F32, tag="peaks", name="peak_of_head")
         nc.vector.tensor_reduce(out=peak_of_head[:], in_=by_point[:], axis=X, op=ALU.max)
         stats = psum_held.tile([D, 2, P], F32, name="stats")
         bias_flipped = held.tile([P, H, DPH], F32, name="bias_flipped")
@@ -84,10 +93,13 @@ def tile_transformerdecoderlayer_equi_v4_kernel(tc, v, dist, wo, tgt, offs, out)
         nc.tensor.transpose(stats[:, 0, :], bias_flipped[:].rearrange("p h r -> p (h r)"), identity[:])
         bias = held.tile([D, P], F32, name="bias")
         nc.scalar.copy(bias[:], stats[:, 0, :])
-        inverse = held.tile([D, P], F32, name="inverse")
+        inverse = [
+            scratch.tile([D, STARTS[2]], F32, tag="inverse_then_agg", name="inverse0"),
+            held.tile([D, P - STARTS[2]], F32, name="inverse1"),
+        ]
 
-        def weigh(k):
-            for p in range(SIZES[k]):
+        def weigh(k, begin):
+            for p in range(begin, SIZES[k]):
                 point = STARTS[k] + p
                 nc.scalar.activation(
                     terms[k][:, T, p, :], logits[k][:, p, :], EXP, bias=bias[:, point : point + 1], scale=0.25
@@ -107,7 +119,15 @@ def tile_transformerdecoderlayer_equi_v4_kernel(tc, v, dist, wo, tgt, offs, out)
             inverse_flipped = held.tile([P, H, DPH], F32, name="inverse_flipped")
             nc.vector.tensor_copy(inverse_flipped[:], inverse_of_head[:].unsqueeze(2).to_broadcast([P, H, DPH]))
             nc.tensor.transpose(stats[:, 1, :], inverse_flipped[:].rearrange("p h r -> p (h r)"), identity[:])
-            nc.scalar.copy(inverse[:], stats[:, 1, :])
+            for i, points in enumerate(pairs):
+                nc.scalar.copy(inverse[i][:], stats[:, 1, points])
+
+        def normalize(k):
+            for p in range(SIZES[k]):
+                column = STARTS[k] - STARTS[2] + p
+                nc.scalar.activation(
+                    terms[k][:, T, p, :], terms[k][:, T, p, :], COPY, scale=inverse[1][:, column : column + 1]
+                )
 
         def look_up(k, t, points):
             nc.vector.tensor_tensor(
@@ -130,47 +150,52 @@ def tile_transformerdecoderlayer_equi_v4_kernel(tc, v, dist, wo, tgt, offs, out)
             sums[k] = psum.tile([D, T, SIZES[k]], F32, name="sums")
             nc.tensor.transpose(sums[k][:].rearrange("d t p -> d (t p)"), flipped_sb[:], identity[0:columns, 0:columns])
 
-        def sum_on_vector(k):
-            sums[k] = work.tile([D, T, SIZES[k]], F32, name="sums_sb")
-            nc.vector.tensor_reduce(out=sums[k][:], in_=terms[k][:, 0:T], axis=X, op=ALU.add)
+        def columns_of(k):
+            begin = STARTS[k] - pairs[k // 2].start
+            return slice(begin, begin + SIZES[k])
 
-        def divide_and_project(first_piece):
-            points = SIZES[first_piece] + SIZES[first_piece + 1]
-            agg = work.tile([D, T, points], BF16, name="agg")
-            for k in (first_piece, first_piece + 1):
-                begin = STARTS[k] - STARTS[first_piece]
-                nc.vector.tensor_tensor(
-                    agg[:, :, begin : begin + SIZES[k]],
-                    sums[k][:],
-                    inverse[:, STARTS[k] : STARTS[k] + SIZES[k]].unsqueeze(1).to_broadcast([D, T, SIZES[k]]),
-                    ALU.mult,
-                )
-            projected[first_piece] = psum.tile([D, T, points], F32, name="projected")
-            nc.tensor.matmul(
-                projected[first_piece][:].rearrange("o t p -> o (t p)"), weights[:], agg[:].rearrange("d t p -> d (t p)")
+        def sum_on_vector(k):
+            with nc.allow_low_precision(reason="agg is rounded once to bfloat16, the sum itself is float32"):
+                nc.vector.tensor_reduce(out=agg[k // 2][:, :, columns_of(k)], in_=terms[k][:, 0:T], axis=X, op=ALU.add)
+
+        def divide(k):
+            nc.vector.tensor_tensor(
+                agg[k // 2][:, :, columns_of(k)],
+                sums[k][:],
+                inverse[k // 2][:, columns_of(k)].unsqueeze(1).to_broadcast([D, T, SIZES[k]]),
+                ALU.mult,
             )
 
-        def add_own_and_store(first_piece):
-            points = slice(STARTS[first_piece], STARTS[first_piece + 1] + SIZES[first_piece + 1])
-            result = work.tile([D, T, points.stop - points.start], F32, name="result")
-            nc.vector.tensor_tensor(result[:], projected[first_piece][:], own[:, :, points], ALU.add)
-            nc.sync.dma_start(out.rearrange("(t o) p -> o t p", o=D)[:, :, points], result[:])
+        def project(i):
+            projected[i] = psum.tile([D, T, pairs[i].stop - pairs[i].start], F32, name="projected")
+            nc.tensor.matmul(
+                projected[i][:].rearrange("o t p -> o (t p)"), weights[:], agg[i][:].rearrange("d t p -> d (t p)")
+            )
 
+        def add_own_and_store(i, queue):
+            result = work.tile([D, T, pairs[i].stop - pairs[i].start], F32, name="result")
+            nc.vector.tensor_tensor(result[:], projected[i][:], own[:, :, pairs[i]], ALU.add)
+            queue.dma_start(out.rearrange("(t o) p -> o t p", o=D)[:, :, pairs[i]], result[:])
+
+        weigh(0, DIRECT_POINTS)
         for k in range(1, PIECES):
-            weigh(k)
+            weigh(k, 0)
         invert_totals()
-        for part in PARTS:
-            for t in range(T):
-                look_up(0, t, part)
-        sum_on_tensor(0)
-        for k in range(1, PIECES):
-            for t in range(T):
-                look_up(k, t, slice(0, SIZES[k]))
-            if k < PIECES - 1:
+        normalize(LAST)
+        for k in range(PIECES):
+            for part in PARTS[k]:
+                for t in range(T):
+                    look_up(k, t, part)
+            if k < LAST:
                 sum_on_tensor(k)
             if k == 2:
-                divide_and_project(0)
-                add_own_and_store(0)
-        sum_on_vector(PIECES - 1)
-        divide_and_project(2)
-        add_own_and_store(2)
+                agg[0] = held.tile([D, T, STARTS[2]], BF16, name="agg0")
+                divide(0)
+                divide(1)
+                project(0)
+        agg[1] = scratch.tile([D, T, P - STARTS[2]], BF16, tag="inverse_then_agg", name="agg1")
+        sum_on_vector(LAST)
+        divide(2)
+        project(1)
+        add_own_and_store(0, nc.scalar)
+        add_own_and_store(1, nc.sync)

@@ -14,18 +14,17 @@ NB = 16
 H = 8
 DPH = D // H
 N = P * NB
-SIZES = [40, 40, 32, 16]
+SIZES = [40, 32, 32, 24]
 STARTS = [sum(SIZES[:k]) for k in range(len(SIZES))]
 PIECES = len(SIZES)
 LAST = PIECES - 1
-PARTS = [
-    [slice(0, 8), slice(8, 16), slice(16, 24), slice(24, 40)],
-    [slice(0, 16), slice(16, 40)],
-    [slice(0, 32)],
-    [slice(0, 16)],
-]
-DIRECT = PARTS[0][:2]
+DIRECT = [slice(0, 8), slice(8, 16)]
 DIRECT_POINTS = DIRECT[-1].stop
+LOOK_UPS = [
+    [(0, part) for part in DIRECT]
+    + [(t, slice(0, DIRECT_POINTS)) for t in range(1, T)]
+    + [(t, slice(DIRECT_POINTS, SIZES[0])) for t in range(T)]
+] + [[(t, slice(0, SIZES[k])) for t in range(T)] for k in range(1, PIECES)]
 
 FLOPS = 2 * T * D * N + 2 * D * D * T * P
 
@@ -183,9 +182,8 @@ def tile_transformerdecoderlayer_equi_v4_kernel(tc, v, dist, wo, tgt, offs, out)
         invert_totals()
         normalize(LAST)
         for k in range(PIECES):
-            for part in PARTS[k]:
-                for t in range(T):
-                    look_up(k, t, part)
+            for t, points in LOOK_UPS[k]:
+                look_up(k, t, points)
             if k < LAST:
                 sum_on_tensor(k)
             if k == 2:

@@ -42,9 +42,9 @@ def tile_transformerdecoderlayer_equi_v4_kernel(tc, v, dist, wo, tgt, offs, out)
         values = [held.tile([D, S], F32, name=f"values{t}") for t in range(T)]
         by_entry = dist.rearrange("d (p n) -> d p n", n=NB)
         nc.sync.dma_start(logits[0][:, 0:DIRECT_POINTS, :], by_entry[:, 0:DIRECT_POINTS, :])
+        nc.sync.dma_start(values[0][:], v[0:D, :])
         by_point = held.tile([P, H, NB], F32, name="by_point")
         nc.scalar.dma_start(by_point[:], dist.rearrange("(h r) (p n) -> r p h n", r=DPH, n=NB)[0])
-        nc.scalar.dma_start(values[0][:], v[0:D, :])
         offsets = held.tile([D, N // 16], U16, name="offsets")
         nc.sync.dma_start(offsets[:], offs)
         nc.sync.dma_start(values[1][:], v[D : 2 * D, :])
@@ -94,7 +94,7 @@ def tile_transformerdecoderlayer_equi_v4_kernel(tc, v, dist, wo, tgt, offs, out)
         nc.scalar.copy(bias[:], stats[:, 0, :])
         inverse = [
             scratch.tile([D, STARTS[2]], F32, tag="inverse_then_agg", name="inverse0"),
-            held.tile([D, P - STARTS[2]], F32, name="inverse1"),
+            scratch.tile([D, P - STARTS[2]], F32, tag="inverse_then_result", name="inverse1"),
         ]
 
         def weigh(k, begin):
@@ -146,7 +146,7 @@ def tile_transformerdecoderlayer_equi_v4_kernel(tc, v, dist, wo, tgt, offs, out)
                 )
             flipped_sb = work.tile([columns, D], F32, name="flipped_sb")
             nc.scalar.copy(flipped_sb[:], flipped[:])
-            sums[k] = psum.tile([D, T, SIZES[k]], F32, name="sums")
+            sums[k] = psum_held.tile([D, T, SIZES[k]], F32, name=f"sums{k}")
             nc.tensor.transpose(sums[k][:].rearrange("d t p -> d (t p)"), flipped_sb[:], identity[0:columns, 0:columns])
 
         def columns_of(k):
@@ -171,10 +171,9 @@ def tile_transformerdecoderlayer_equi_v4_kernel(tc, v, dist, wo, tgt, offs, out)
                 projected[i][:].rearrange("o t p -> o (t p)"), weights[:], agg[i][:].rearrange("d t p -> d (t p)")
             )
 
-        def add_own_and_store(i, queue):
-            result = work.tile([D, T, pairs[i].stop - pairs[i].start], F32, name="result")
+        def add_own_and_store(i, result):
             nc.vector.tensor_tensor(result[:], projected[i][:], own[:, :, pairs[i]], ALU.add)
-            queue.dma_start(out.rearrange("(t o) p -> o t p", o=D)[:, :, pairs[i]], result[:])
+            nc.sync.dma_start(out.rearrange("(t o) p -> o t p", o=D)[:, :, pairs[i]], result[:])
 
         weigh(0, DIRECT_POINTS)
         for k in range(1, PIECES):
@@ -192,8 +191,12 @@ def tile_transformerdecoderlayer_equi_v4_kernel(tc, v, dist, wo, tgt, offs, out)
                 divide(1)
                 project(0)
         agg[1] = scratch.tile([D, T, P - STARTS[2]], BF16, tag="inverse_then_agg", name="agg1")
-        sum_on_vector(LAST)
         divide(2)
+        sum_on_vector(LAST)
         project(1)
-        add_own_and_store(0, nc.scalar)
-        add_own_and_store(1, nc.sync)
+        result = [
+            scratch.tile([D, T, STARTS[2]], F32, tag="inverse_then_result", name="result0"),
+            held.tile([D, T, P - STARTS[2]], F32, name="result1"),
+        ]
+        for i in range(len(pairs)):
+            add_own_and_store(i, result[i])

@@ -71,15 +71,18 @@ def tile_transformerdecoderlayer_equi_v4_kernel(tc, v, dist, wo, tgt, offs, out)
         agg = [None] * len(pairs)
         projected = [None] * len(pairs)
 
-        first_peaks = scratch.tile([D, DIRECT_POINTS], F32, tag="peaks", name="first_peaks")
+        first_peaks = [
+            scratch.tile([D, DIRECT[0].stop], F32, tag="peaks", name="first_peaks0"),
+            held.tile([D, DIRECT_POINTS - DIRECT[0].stop], F32, name="first_peaks1"),
+        ]
         shifted = scratch.tile([D, DIRECT_POINTS, NB], F32, tag="scratch", name="shifted")
-        for part in DIRECT:
-            nc.vector.tensor_reduce(out=first_peaks[:, part], in_=logits[0][:, part, :], axis=X, op=ALU.max)
-        for part in DIRECT:
+        for part, peaks in zip(DIRECT, first_peaks):
+            nc.vector.tensor_reduce(out=peaks[:], in_=logits[0][:, part, :], axis=X, op=ALU.max)
+        for part, peaks in zip(DIRECT, first_peaks):
             nc.vector.tensor_tensor(
                 shifted[:, part, :],
                 logits[0][:, part, :],
-                first_peaks[:, part].unsqueeze(2).to_broadcast([D, part.stop - part.start, NB]),
+                peaks[:].unsqueeze(2).to_broadcast([D, part.stop - part.start, NB]),
                 ALU.subtract,
             )
             nc.scalar.activation(terms[0][:, T, part, :], shifted[:, part, :], EXP, scale=0.25)

@@ -41,12 +41,13 @@ def tile_transformerdecoderlayer_equi_v4_kernel(tc, v, dist, wo, tgt, offs, out)
         logits = [held.tile([D, SIZES[k], NB], F32, name=f"logits{k}") for k in range(PIECES)]
         values = [held.tile([D, S], F32, name=f"values{t}") for t in range(T)]
         by_entry = dist.rearrange("d (p n) -> d p n", n=NB)
-        nc.sync.dma_start(logits[0][:, 0:DIRECT_POINTS, :], by_entry[:, 0:DIRECT_POINTS, :])
-        nc.sync.dma_start(values[0][:], v[0:D, :])
-        by_point = held.tile([P, H, NB], F32, name="by_point")
-        nc.scalar.dma_start(by_point[:], dist.rearrange("(h r) (p n) -> r p h n", r=DPH, n=NB)[0])
+        for part in DIRECT:
+            nc.sync.dma_start(logits[0][:, part, :], by_entry[:, part, :])
         offsets = held.tile([D, N // 16], U16, name="offsets")
         nc.sync.dma_start(offsets[:], offs)
+        by_point = held.tile([P, H, NB], F32, name="by_point")
+        nc.sync.dma_start(by_point[:], dist.rearrange("(h r) (p n) -> r p h n", r=DPH, n=NB)[0])
+        nc.sync.dma_start(values[0][:], v[0:D, :])
         nc.sync.dma_start(values[1][:], v[D : 2 * D, :])
         nc.sync.dma_start(logits[0][:, DIRECT_POINTS : SIZES[0], :], by_entry[:, DIRECT_POINTS : SIZES[0], :])
         nc.sync.dma_start(values[2][:], v[2 * D : 3 * D, :])
@@ -66,7 +67,10 @@ def tile_transformerdecoderlayer_equi_v4_kernel(tc, v, dist, wo, tgt, offs, out)
         nc.scalar.activation(one[:], zero[:], EXP)
 
         terms = [held.tile([D, T + 1, SIZES[k], NB], F32, name=f"terms{k}") for k in range(PIECES)]
-        sums = [None] * PIECES
+        first_sums = psum_held.tile([D, T * STARTS[2]], F32, name="first_sums")
+        sums = [first_sums[:, T * STARTS[k] : T * STARTS[k + 1]] for k in range(2)]
+        last_sums = psum_held.tile([D, T * SIZES[2]], F32, name="last_sums")
+        sums.append(last_sums[:])
         pairs = [slice(0, STARTS[2]), slice(STARTS[2], P)]
         agg = [None] * len(pairs)
         projected = [None] * len(pairs)
@@ -96,7 +100,7 @@ def tile_transformerdecoderlayer_equi_v4_kernel(tc, v, dist, wo, tgt, offs, out)
         bias = held.tile([D, P], F32, name="bias")
         nc.scalar.copy(bias[:], stats[:, 0, :])
         inverse = [
-            scratch.tile([D, STARTS[2]], F32, tag="inverse_then_agg", name="inverse0"),
+            scratch.tile([D, T * STARTS[2]], F32, tag="inverse_then_agg", name="inverse0"),
             scratch.tile([D, P - STARTS[2]], F32, tag="inverse_then_result", name="inverse1"),
         ]
 
@@ -121,8 +125,11 @@ def tile_transformerdecoderlayer_equi_v4_kernel(tc, v, dist, wo, tgt, offs, out)
             inverse_flipped = held.tile([P, H, DPH], F32, name="inverse_flipped")
             nc.vector.tensor_copy(inverse_flipped[:], inverse_of_head[:].unsqueeze(2).to_broadcast([P, H, DPH]))
             nc.tensor.transpose(stats[:, 1, :], inverse_flipped[:].rearrange("p h r -> p (h r)"), identity[:])
-            for i, points in enumerate(pairs):
-                nc.scalar.copy(inverse[i][:], stats[:, 1, points])
+            for k in range(2):
+                by_component = inverse[0][:, T * STARTS[k] : T * STARTS[k + 1]].rearrange("d (t p) -> d t p", t=T)
+                inverses = stats[:, 1, STARTS[k] : STARTS[k + 1]]
+                nc.scalar.copy(by_component, inverses.unsqueeze(1).to_broadcast([D, T, SIZES[k]]))
+            nc.scalar.copy(inverse[1][:], stats[:, 1, pairs[1]])
 
         def normalize(k):
             for p in range(SIZES[k]):
@@ -149,29 +156,38 @@ def tile_transformerdecoderlayer_equi_v4_kernel(tc, v, dist, wo, tgt, offs, out)
                 )
             flipped_sb = work.tile([columns, D], F32, name="flipped_sb")
             nc.scalar.copy(flipped_sb[:], flipped[:])
-            sums[k] = psum_held.tile([D, T, SIZES[k]], F32, name=f"sums{k}")
-            nc.tensor.transpose(sums[k][:].rearrange("d t p -> d (t p)"), flipped_sb[:], identity[0:columns, 0:columns])
+            nc.tensor.transpose(sums[k], flipped_sb[:], identity[0:columns, 0:columns])
 
         def columns_of(k):
             begin = STARTS[k] - pairs[k // 2].start
             return slice(begin, begin + SIZES[k])
 
-        def sum_on_vector(k):
+        def average_last(components):
             with nc.allow_low_precision(reason="agg is rounded once to bfloat16, the sum itself is float32"):
-                nc.vector.tensor_reduce(out=agg[k // 2][:, :, columns_of(k)], in_=terms[k][:, 0:T], axis=X, op=ALU.add)
+                nc.vector.tensor_reduce(
+                    out=agg[1][:, components, columns_of(LAST)], in_=terms[LAST][:, components], axis=X, op=ALU.add
+                )
 
-        def divide(k):
+        def project_first_pair():
+            nc.vector.tensor_tensor(agg[0][:], first_sums[:], inverse[0][:], ALU.mult)
+            projected[0] = psum.tile([D, T, STARTS[2]], F32, name="projected")
+            for k in range(2):
+                nc.tensor.matmul(
+                    projected[0][:, :, columns_of(k)],
+                    weights[:],
+                    agg[0][:, T * STARTS[k] : T * STARTS[k + 1]].rearrange("d (t p) -> d t p", t=T),
+                )
+
+        def project_second_pair():
             nc.vector.tensor_tensor(
-                agg[k // 2][:, :, columns_of(k)],
-                sums[k][:],
-                inverse[k // 2][:, columns_of(k)].unsqueeze(1).to_broadcast([D, T, SIZES[k]]),
+                agg[1][:, :, columns_of(2)],
+                sums[2].rearrange("d (t p) -> d t p", t=T),
+                inverse[1][:, columns_of(2)].unsqueeze(1).to_broadcast([D, T, SIZES[2]]),
                 ALU.mult,
             )
-
-        def project(i):
-            projected[i] = psum.tile([D, T, pairs[i].stop - pairs[i].start], F32, name="projected")
+            projected[1] = psum.tile([D, T, P - STARTS[2]], F32, name="projected")
             nc.tensor.matmul(
-                projected[i][:].rearrange("o t p -> o (t p)"), weights[:], agg[i][:].rearrange("d t p -> d (t p)")
+                projected[1][:].rearrange("o t p -> o (t p)"), weights[:], agg[1][:].rearrange("d t p -> d (t p)")
             )
 
         def add_own_and_store(i, result):
@@ -189,14 +205,12 @@ def tile_transformerdecoderlayer_equi_v4_kernel(tc, v, dist, wo, tgt, offs, out)
             if k < LAST:
                 sum_on_tensor(k)
             if k == 2:
-                agg[0] = held.tile([D, T, STARTS[2]], BF16, name="agg0")
-                divide(0)
-                divide(1)
-                project(0)
+                agg[0] = held.tile([D, T * STARTS[2]], BF16, name="agg0")
+                project_first_pair()
         agg[1] = scratch.tile([D, T, P - STARTS[2]], BF16, tag="inverse_then_agg", name="agg1")
-        divide(2)
-        sum_on_vector(LAST)
-        project(1)
+        average_last(slice(0, T - 1))
+        average_last(slice(T - 1, T))
+        project_second_pair()
         result = [
             scratch.tile([D, T, STARTS[2]], F32, tag="inverse_then_result", name="result0"),
             held.tile([D, T, P - STARTS[2]], F32, name="result1"),

@@ -46,7 +46,7 @@ def tile_transformerdecoderlayer_equi_v4_kernel(tc, v, dist, wo, tgt, offs, out)
         offsets = held.tile([D, N // 16], U16, name="offsets")
         nc.sync.dma_start(offsets[:], offs)
         by_point = held.tile([P, H, NB], F32, name="by_point")
-        nc.sync.dma_start(by_point[:], dist.rearrange("(h r) (p n) -> r p h n", r=DPH, n=NB)[0])
+        nc.scalar.dma_start(by_point[:], dist.rearrange("(h r) (p n) -> r p h n", r=DPH, n=NB)[0])
         nc.sync.dma_start(values[0][:], v[0:D, :])
         nc.sync.dma_start(values[1][:], v[D : 2 * D, :])
         nc.sync.dma_start(logits[0][:, DIRECT_POINTS : SIZES[0], :], by_entry[:, DIRECT_POINTS : SIZES[0], :])

import concourse.mybir as mybir
from concourse.masks import make_identity

F32, BF16, U16 = mybir.dt.float32, mybir.dt.bfloat16, mybir.dt.uint16
ALU = mybir.AluOpType
X = mybir.AxisListType.X
EXP, COPY = mybir.ActivationFunctionType.Exp, mybir.ActivationFunctionType.Copy

D = 128
T = 3
S = 512
P = 128
NB = 16
H = 8
DPH = D // H
N = P * NB
SIZES = [40, 32, 32, 24]
STARTS = [sum(SIZES[:k]) for k in range(len(SIZES))]
PIECES = len(SIZES)
LAST = PIECES - 1
DIRECT = [slice(0, 8), slice(8, 16)]
DIRECT_POINTS = DIRECT[-1].stop
LOOK_UPS = [
    [(0, part) for part in DIRECT]
    + [(t, slice(0, DIRECT_POINTS)) for t in range(1, T)]
    + [(t, slice(DIRECT_POINTS, SIZES[0])) for t in range(T)]
] + [[(t, slice(0, SIZES[k])) for t in range(T)] for k in range(1, PIECES)]

FLOPS = 2 * T * D * N + 2 * D * D * T * P


def tile_transformerdecoderlayer_equi_v4_kernel(tc, v, dist, wo, tgt, offs, out):
    nc = tc.nc
    with (
        tc.tile_pool(name="held", bufs=1) as held,
        tc.tile_pool(name="scratch", bufs=1) as scratch,
        tc.tile_pool(name="work", bufs=2) as work,
        tc.psum_pool(name="psum", bufs=2) as psum,
        tc.psum_pool(name="psum_held", bufs=1) as psum_held,
    ):
        logits = [held.tile([D, SIZES[k], NB], F32, name=f"logits{k}") for k in range(PIECES)]
        values = [held.tile([D, S], F32, name=f"values{t}") for t in range(T)]
        by_entry = dist.rearrange("d (p n) -> d p n", n=NB)
        for part in DIRECT:
            nc.sync.dma_start(logits[0][:, part, :], by_entry[:, part, :])
        offsets = held.tile([D, N // 16], U16, name="offsets")
        nc.sync.dma_start(offsets[:], offs)
        by_point = held.tile([P, H, NB], F32, name="by_point")
        nc.scalar.dma_start(by_point[:], dist.rearrange("(h r) (p n) -> r p h n", r=DPH, n=NB)[0])
        nc.sync.dma_start(values[0][:], v[0:D, :])
        nc.sync.dma_start(values[1][:], v[D : 2 * D, :])
        nc.sync.dma_start(logits[0][:, DIRECT_POINTS : SIZES[0], :], by_entry[:, DIRECT_POINTS : SIZES[0], :])
        nc.sync.dma_start(values[2][:], v[2 * D : 3 * D, :])
        for k in range(1, PIECES):
            nc.sync.dma_start(logits[k][:], by_entry[:, STARTS[k] : STARTS[k] + SIZES[k], :])
        own = held.tile([D, T, P], F32, name="own")
        nc.sync.dma_start(own[:], tgt.rearrange("(t o) p -> o t p", o=D))
        weights = held.tile([D, D], BF16, name="weights")
        nc.sync.dma_start(weights[:], wo)

        identity = held.tile([D, D], F32, name="identity")
        make_identity(nc, identity[:])

        zero = held.tile([D, 1], F32, name="zero")
        nc.vector.memset(zero[:], 0.0)
        one = held.tile([D, 1], F32, name="one")
        nc.scalar.activation(one[:], zero[:], EXP)

        terms = [held.tile([D, T + 1, SIZES[k], NB], F32, name=f"terms{k}") for k in range(PIECES)]
        first_sums = psum_held.tile([D, T * STARTS[2]], F32, name="first_sums")
        sums = [first_sums[:, T * STARTS[k] : T * STARTS[k + 1]] for k in range(2)]
        last_sums = psum_held.tile([D, T * SIZES[2]], F32, name="last_sums")
        sums.append(last_sums[:])
        pairs = [slice(0, STARTS[2]), slice(STARTS[2], P)]
        agg = [None] * len(pairs)
        projected = [None] * len(pairs)

        first_peaks = [
            scratch.tile([D, DIRECT[0].stop], F32, tag="peaks", name="first_peaks0"),
            held.tile([D, DIRECT_POINTS - DIRECT[0].stop], F32, name="first_peaks1"),
        ]
        shifted = scratch.tile([D, DIRECT_POINTS, NB], F32, tag="scratch", name="shifted")
        for part, peaks in zip(DIRECT, first_peaks):
            nc.vector.tensor_reduce(out=peaks[:], in_=logits[0][:, part, :], axis=X, op=ALU.max)
        for part, peaks in zip(DIRECT, first_peaks):
            nc.vector.tensor_tensor(
                shifted[:, part, :],
                logits[0][:, part, :],
                peaks[:].unsqueeze(2).to_broadcast([D, part.stop - part.start, NB]),
                ALU.subtract,
            )
            nc.scalar.activation(terms[0][:, T, part, :], shifted[:, part, :], EXP, scale=0.25)

        peak_of_head = scratch.tile([P, H], F32, tag="peaks", name="peak_of_head")
        nc.vector.tensor_reduce(out=peak_of_head[:], in_=by_point[:], axis=X, op=ALU.max)
        stats = psum_held.tile([D, 2, P], F32, name="stats")
        bias_flipped = held.tile([P, H, DPH], F32, name="bias_flipped")
        nc.vector.tensor_scalar_mul(bias_flipped[:], peak_of_head[:].unsqueeze(2).to_broadcast([P, H, DPH]), -0.25)
        nc.tensor.transpose(stats[:, 0, :], bias_flipped[:].rearrange("p h r -> p (h r)"), identity[:])
        bias = held.tile([D, P], F32, name="bias")
        nc.scalar.copy(bias[:], stats[:, 0, :])
        inverse = [
            scratch.tile([D, T * STARTS[2]], F32, tag="inverse_then_agg", name="inverse0"),
            scratch.tile([D, P - STARTS[2]], F32, tag="inverse_then_result", name="inverse1"),
        ]

        def weigh(k, begin):
            for p in range(begin, SIZES[k]):
                point = STARTS[k] + p
                nc.scalar.activation(
                    terms[k][:, T, p, :], logits[k][:, p, :], EXP, bias=bias[:, point : point + 1], scale=0.25
                )

        def invert_totals():
            shifted_by_point = held.tile([P, H, NB], F32, name="shifted_by_point")
            nc.vector.tensor_tensor(
                shifted_by_point[:], by_point[:], peak_of_head[:].unsqueeze(2).to_broadcast([P, H, NB]), ALU.subtract
            )
            weight_by_point = scratch.tile([P, H, NB], F32, tag="scratch", name="weight_by_point")
            nc.scalar.activation(weight_by_point[:], shifted_by_point[:], EXP, scale=0.25)
            total_of_head = held.tile([P, H], F32, name="total_of_head")
            nc.vector.tensor_reduce(out=total_of_head[:], in_=weight_by_point[:], axis=X, op=ALU.add)
            inverse_of_head = held.tile([P, H], F32, name="inverse_of_head")
            nc.vector.reciprocal(inverse_of_head[:], total_of_head[:])
            inverse_flipped = held.tile([P, H, DPH], F32, name="inverse_flipped")
            nc.vector.tensor_copy(inverse_flipped[:], inverse_of_head[:].unsqueeze(2).to_broadcast([P, H, DPH]))
            nc.tensor.transpose(stats[:, 1, :], inverse_flipped[:].rearrange("p h r -> p (h r)"), identity[:])
            for k in range(2):
                by_component = inverse[0][:, T * STARTS[k] : T * STARTS[k + 1]].rearrange("d (t p) -> d t p", t=T)
                inverses = stats[:, 1, STARTS[k] : STARTS[k + 1]]
                nc.scalar.copy(by_component, inverses.unsqueeze(1).to_broadcast([D, T, SIZES[k]]))
            nc.scalar.copy(inverse[1][:], stats[:, 1, pairs[1]])

        def normalize(k):
            for p in range(SIZES[k]):
                column = STARTS[k] - STARTS[2] + p
                nc.scalar.activation(
                    terms[k][:, T, p, :], terms[k][:, T, p, :], COPY, scale=inverse[1][:, column : column + 1]
                )

        def look_up(k, t, points):
            nc.vector.tensor_tensor(
                terms[k][:, t, points, :].rearrange("d p n -> d (p n)"),
                values[t][:].indirect(offsets[:, STARTS[k] + points.start : STARTS[k] + points.stop]),
                terms[k][:, T, points, :].rearrange("d p n -> d (p n)"),
                ALU.mult,
            )

        def sum_on_tensor(k):
            columns = T * SIZES[k]
            by_neighbour = terms[k][:, 0:T].rearrange("d t p n -> d (t p) n")
            flipped = psum.tile([columns, D], F32, name="flipped")
            for n in range(NB):
                nc.tensor.matmul(
                    flipped[:], by_neighbour[:, :, n], identity[:], is_transpose=True, start=(n == 0), stop=(n == NB - 1)
                )
            flipped_sb = work.tile([columns, D], F32, name="flipped_sb")
            nc.scalar.copy(flipped_sb[:], flipped[:])
            nc.tensor.transpose(sums[k], flipped_sb[:], identity[0:columns, 0:columns])

        def columns_of(k):
            begin = STARTS[k] - pairs[k // 2].start
            return slice(begin, begin + SIZES[k])

        def average_last(components):
            with nc.allow_low_precision(reason="agg is rounded once to bfloat16, the sum itself is float32"):
                nc.vector.tensor_reduce(
                    out=agg[1][:, components, columns_of(LAST)], in_=terms[LAST][:, components], axis=X, op=ALU.add
                )

        def project_first_pair():
            nc.vector.tensor_tensor(agg[0][:], first_sums[:], inverse[0][:], ALU.mult)
            projected[0] = psum.tile([D, T, STARTS[2]], F32, name="projected")
            for k in range(2):
                nc.tensor.matmul(
                    projected[0][:, :, columns_of(k)],
                    weights[:],
                    agg[0][:, T * STARTS[k] : T * STARTS[k + 1]].rearrange("d (t p) -> d t p", t=T),
                )

        def project_second_pair():
            nc.vector.tensor_tensor(
                agg[1][:, :, columns_of(2)],
                sums[2].rearrange("d (t p) -> d t p", t=T),
                inverse[1][:, columns_of(2)].unsqueeze(1).to_broadcast([D, T, SIZES[2]]),
                ALU.mult,
            )
            projected[1] = psum.tile([D, T, P - STARTS[2]], F32, name="projected")
            nc.tensor.matmul(
                projected[1][:].rearrange("o t p -> o (t p)"), weights[:], agg[1][:].rearrange("d t p -> d (t p)")
            )

        def add_own_and_store(i, result):
            nc.vector.tensor_tensor(result[:], projected[i][:], own[:, :, pairs[i]], ALU.add)
            nc.sync.dma_start(out.rearrange("(t o) p -> o t p", o=D)[:, :, pairs[i]], result[:])

        weigh(0, DIRECT_POINTS)
        for k in range(1, PIECES):
            weigh(k, 0)
        invert_totals()
        normalize(LAST)
        for k in range(PIECES):
            for t, points in LOOK_UPS[k]:
                look_up(k, t, points)
            if k < LAST:
                sum_on_tensor(k)
            if k == 2:
                agg[0] = held.tile([D, T * STARTS[2]], BF16, name="agg0")
                project_first_pair()
        agg[1] = scratch.tile([D, T, P - STARTS[2]], BF16, tag="inverse_then_agg", name="agg1")
        average_last(slice(0, T - 1))
        average_last(slice(T - 1, T))
        project_second_pair()
        result = [
            scratch.tile([D, T, STARTS[2]], F32, tag="inverse_then_result", name="result0"),
            held.tile([D, T, P - STARTS[2]], F32, name="result1"),
        ]
        for i in range(len(pairs)):
            add_own_and_store(i, result[i])
